import numpy as np
import ml_dtypes


def mxq(x, axis, fmt="e4m3"):
    dtype, down = {"e4m3": (ml_dtypes.float8_e4m3fn, 7), "e5m2": (ml_dtypes.float8_e5m2, 14)}[fmt]
    v = np.moveaxis(np.asarray(x, np.float32).astype(ml_dtypes.bfloat16).astype(np.float64), axis, -1)
    blocks = v.reshape(v.shape[:-1] + (-1, 32))
    amax = np.abs(blocks).max(-1, keepdims=True)
    byte = np.maximum(np.where(amax > 0, np.frexp(amax)[1] - 1 + 127, 0) - down, 1)
    scale = np.exp2(byte - 127.0)
    codes = (blocks / scale).astype(np.float32).astype(dtype).astype(np.float64)
    return np.moveaxis((codes * scale).reshape(v.shape), -1, axis)


WIDE = False


def mx_kscale(k):
    if not WIDE:
        return np.ones(k)
    levels = np.array([10, -10, 5, -5, 0])
    a = np.random.permutation(np.resize(levels, k // 512 * 4)).reshape(k // 512, 4)
    idx = np.arange(k)
    return np.exp2(a[idx // 512, idx % 128 // 32])


BF16 = ml_dtypes.bfloat16


def bf(x):
    return np.asarray(x, np.float32).astype(BF16)


def f64(x):
    return np.asarray(x).astype(np.float64)


E2M1 = np.array([0.0, 0.5, 1.0, 1.5, 2.0, 3.0, 4.0, 6.0, -0.0, -0.5, -1.0, -1.5, -2.0, -3.0, -4.0, -6.0])


def pack_weight(w, fmt):
    k, n = w.shape
    w = f64(bf(w)).reshape(k // 32, 32, n)
    amax = np.abs(w).max(1)
    if fmt == "e4m3":
        byte = np.frexp(amax)[1] - 1 + 127 - 7
    else:
        mant, ex = np.frexp(amax / 6.0)
        byte = np.where(mant > 0.5, ex, ex - 1) + 127
    byte = np.clip(np.where(amax > 0, byte, 1), 1, 254)
    scaled = (w * np.exp2(127.0 - byte)[:, None, :]).reshape(k, n).astype(np.float32)
    by_word = np.ascontiguousarray(scaled.reshape(k // 512, 128, 4, n).transpose(0, 1, 3, 2))
    if fmt == "e4m3":
        words = by_word.astype(ml_dtypes.float8_e4m3fn).view(np.uint8)
    else:
        c = by_word.astype(ml_dtypes.float4_e2m1fn).view(np.uint8) & 0xF
        words = c[..., 0::2] | (c[..., 1::2] << 4)
    return np.ascontiguousarray(words), np.ascontiguousarray(byte.astype(np.uint8).reshape(k // 512, 16, n))


def unpack_weight(words, scales, fmt):
    g, p, n, _ = words.shape
    if fmt == "e4m3":
        vals = np.ascontiguousarray(words).view(ml_dtypes.float8_e4m3fn).astype(np.float64)
    else:
        nib = np.empty((g, p, n, 4), np.uint8)
        nib[..., 0::2] = words & 0xF
        nib[..., 1::2] = words >> 4
        vals = E2M1[nib]
    vals = vals * np.repeat(np.exp2(scales.astype(np.float64) - 127.0), 8, axis=1)[..., None]
    return vals.transpose(0, 1, 3, 2).reshape(g * 512, n)

def pack4(w):
    words, scales = pack_weight(w, "e2m1")
    return words.reshape(words.shape[0], 128, -1), scales


def unpack4(words, scales):
    return unpack_weight(words.reshape(words.shape[0], 128, -1, 2), scales, "e2m1")


B, S, DIM, H, NOPE, ROPE, VHD, KV_RANK = 2, 256, 2048, 16, 128, 64, 128, 512
QKHD = NOPE + ROPE
HALF = ROPE // 2


def rope(u, cos, sin):
    ur = u.reshape(u.shape[:-1] + (HALF, 2))
    a, b = ur[..., 0], ur[..., 1]
    c = cos[None, :, None, :]
    s = sin[None, :, None, :]
    return np.stack([a * c - b * s, a * s + b * c], axis=-1).reshape(u.shape)


def setup_inputs():
    s = mx_kscale(DIM)
    inv_freq = 1.0 / 10000.0 ** (np.arange(0, ROPE, 2) / ROPE)
    ang = np.arange(S)[:, None] * inv_freq[None, :]
    x = bf(np.random.standard_normal((B, S, DIM)) * s)
    wq_w_words, wq_w_scales = pack4(np.random.standard_normal((DIM, H * QKHD)) / np.sqrt(DIM) / s[:, None])
    return {"x": x,
            "wq_w_words": wq_w_words, "wq_w_scales": wq_w_scales,
            "wq_b": bf(np.random.standard_normal(H * QKHD) * 0.2),
            "cos": bf(np.cos(ang)), "sin": bf(np.sin(ang))}


def reference(x, wq_w_words, wq_w_scales, wq_b, cos, sin):
    q = (mxq(f64(x), 2, "e4m3") @ unpack4(wq_w_words, wq_w_scales)) + f64(wq_b)
    q = q.reshape(B, S, H, QKHD)
    return np.concatenate([q[..., :NOPE], rope(q[..., NOPE:], f64(cos), f64(sin))], axis=-1)

@@ -1,0 +1,166 @@
+from contextlib import ExitStack
+
+import concourse.mybir as mybir
+from concourse.masks import make_identity
+
+F32 = mybir.dt.float32
+BF16 = mybir.dt.bfloat16
+I32 = mybir.dt.int32
+U32 = mybir.dt.uint32
+U8 = mybir.dt.uint8
+FP8X4 = mybir.dt.float8_e4m3fn_x4
+FP4X4 = mybir.dt.float4_e2m1fn_x4
+ADD = mybir.AluOpType.add
+MULT = mybir.AluOpType.mult
+
+P = 128
+BATCH, SEQ, DIM = 2, 256, 2048
+HEADS, HEAD_DIM = 16, 192
+N_OUT = HEADS * HEAD_DIM
+TOKEN_TILES = BATCH * SEQ // P
+SEQ_TILES = SEQ // P
+K_PASS = 4 * P
+PASSES = DIM // K_PASS
+BLOCK = 512
+BLOCKS = N_OUT // BLOCK
+UNIT = 64
+UNITS = BLOCK // UNIT
+MAX_ROT = 3
+HALF = UNIT // 2
+
+FLOPS = 2 * BATCH * SEQ * DIM * N_OUT
+
+
+def tile_mla_pb_kernel(tc, x, wq_w_words, wq_w_scales, wq_b, cos, sin, out):
+    nc = tc.nc
+    x_rows = x.flatten_outer_dims()
+    out_rows = out.rearrange("b s h d -> b s (h d)")
+
+    with ExitStack() as ctx:
+        keep = ctx.enter_context(tc.tile_pool(name="keep", bufs=1))
+        results = ctx.enter_context(tc.tile_pool(name="results", bufs=BLOCKS * BATCH))
+        banks = ctx.enter_context(tc.psum_pool(name="banks", bufs=8))
+
+        x_sb = keep.tile([P, TOKEN_TILES, DIM], BF16)
+        x_grouped = keep.tile([P, TOKEN_TILES, PASSES * P * 4], BF16, align_bytes=64)
+        x_codes = keep.tile([P, TOKEN_TILES, PASSES * P], U32, align_bytes=64)
+        x_scales = keep.tile([P, TOKEN_TILES, PASSES * P], U8, align_bytes=64)
+        w_words = keep.tile([P, PASSES, 2 * N_OUT], U8, align_bytes=64)
+        w_scales = keep.tile([P, PASSES, N_OUT], U8, align_bytes=64)
+        bias_rows = keep.tile([P, BLOCK], BF16)
+        bias_all = keep.tile([P, N_OUT], F32)
+        ident_f32 = keep.tile([P, P], F32)
+        ident_bf16 = keep.tile([P, P], BF16)
+        cos_sb = keep.tile([P, SEQ_TILES, HALF], BF16)
+        sin_sb = keep.tile([P, SEQ_TILES, HALF], BF16)
+        cos_pairs = keep.tile([P, SEQ_TILES, HALF, 2], F32)
+        sin_pairs = keep.tile([P, SEQ_TILES, HALF, 2], F32)
+
+        nc.vector.memset(w_scales[:].bitcast(I32), 0)
+        nc.vector.memset(bias_rows[:], 0.0)
+        make_identity(nc, ident_f32[:])
+        make_identity(nc, ident_bf16[:])
+
+        nc.scalar.dma_start(out=bias_rows[0:BLOCKS, :], in_=wq_b.rearrange("(r c) -> r c", c=BLOCK))
+        nc.scalar.dma_start(out=cos_sb[:], in_=cos.rearrange("(t p) j -> p t j", p=P))
+        nc.scalar.dma_start(out=sin_sb[:], in_=sin.rearrange("(t p) j -> p t j", p=P))
+
+        for m in range(TOKEN_TILES):
+            nc.sync.dma_start(out=x_sb[:, m, :], in_=x_rows[m * P : (m + 1) * P, :])
+
+        for nb in range(BLOCKS):
+            cols = slice(nb * BLOCK, (nb + 1) * BLOCK)
+            for r in range(4):
+                nc.sync.dma_start(
+                    out=w_scales[r:P:32, :, cols].bitcast(I32),
+                    in_=wq_w_scales[:, r:16:4, cols].bitcast(I32).rearrange("g q n -> q g n"),
+                )
+            word_bytes = slice(2 * nb * BLOCK, 2 * (nb + 1) * BLOCK)
+            nc.sync.dma_start(
+                out=w_words[:, :, word_bytes].bitcast(I32),
+                in_=wq_w_words[:, :, word_bytes].bitcast(I32).rearrange("g p b -> p g b"),
+            )
+
+        nc.vector.tensor_copy(
+            out=cos_pairs[:], in_=cos_sb[:].unsqueeze(3).to_broadcast([P, SEQ_TILES, HALF, 2])
+        )
+        nc.vector.tensor_scalar_mul(out=sin_pairs[:, :, :, 0], in0=sin_sb[:], scalar1=-1.0)
+        nc.vector.tensor_copy(out=sin_pairs[:, :, :, 1], in_=sin_sb[:])
+
+        for r in range(BLOCKS):
+            bias_bank = banks.tile([P, BLOCK], F32, tag="bank")
+            nc.tensor.matmul(
+                out=bias_bank[:],
+                lhsT=ident_bf16[:, r : r + 1].to_broadcast([P, P]),
+                rhs=bias_rows[:],
+                start=True,
+                stop=True,
+            )
+            nc.scalar.copy(out=bias_all[:, r * BLOCK : (r + 1) * BLOCK], in_=bias_bank[:])
+
+        x_words = x_sb[:].bitcast(F32)
+        grouped_words = x_grouped[:].bitcast(F32)
+        for m in range(TOKEN_TILES):
+            for half in range(PASSES // 2):
+                turned = banks.tile([P, 4, P], F32, tag="bank")
+                for i in range(4):
+                    g, u = 2 * half + i // 2, i % 2
+                    nc.tensor.transpose(
+                        turned[:, i, :],
+                        x_words[:, m, 256 * g + u : 256 * (g + 1) : 2],
+                        ident_f32[:],
+                    )
+                dst = grouped_words[:, m, 512 * half : 512 * (half + 1)].rearrange(
+                    "p (g r u) -> p g r u", g=2, u=2
+                )
+                src = turned[:].rearrange("p (g u) r -> p g r u", u=2)
+                if half == 0:
+                    nc.vector.tensor_copy(out=dst, in_=src)
+                else:
+                    nc.scalar.copy(out=dst, in_=src)
+            nc.vector.quantize_mx(
+                out=x_codes[:, m, :].bitcast(FP8X4),
+                scales=x_scales[:, m, :],
+                in_=x_grouped[:, m, :],
+            )
+
+        for nb in range(BLOCKS):
+            cols = slice(nb * BLOCK, (nb + 1) * BLOCK)
+            word_bytes = slice(2 * nb * BLOCK, 2 * (nb + 1) * BLOCK)
+            first = (2 - UNITS * nb) % 3
+            n_rot = len(range(first, UNITS, 3))
+            for b in range(BATCH):
+                q = results.tile([P, SEQ_TILES, BLOCK], F32)
+                for t in range(SEQ_TILES):
+                    m = b * SEQ_TILES + t
+                    acc = banks.tile([P, BLOCK], F32, tag="bank")
+                    for g in range(PASSES):
+                        toks = slice(g * P, (g + 1) * P)
+                        nc.tensor.matmul_mx(
+                            out=acc[:],
+                            lhsT=x_codes[:, m, toks].bitcast(FP8X4),
+                            lhsT_scale=x_scales[:, m, toks],
+                            rhs=w_words[:, g, word_bytes].bitcast(FP4X4),
+                            rhs_scale=w_scales[:, g, cols],
+                            start=(g == 0),
+                            stop=(g == PASSES - 1),
+                        )
+                    nc.vector.tensor_tensor(out=q[:, t, :], in0=acc[:], in1=bias_all[:, cols], op=ADD)
+
+                rotated = q[:].rearrange("p t (u c) -> p t u c", c=UNIT)[:, :, first:UNITS:3, :]
+                pairs = q[:].rearrange("p t (u j e) -> p t u j e", j=HALF, e=2)[:, :, first:UNITS:3, :, :]
+                swapped_full = results.tile([P, SEQ_TILES, MAX_ROT, UNIT], F32)
+                swapped = swapped_full[:, :, 0:n_rot, :]
+                swapped_pairs = swapped.rearrange("p t h (j e) -> p t h j e", e=2)
+                shape = [P, SEQ_TILES, n_rot, UNIT]
+                cos_bc = cos_pairs[:].rearrange("p t j e -> p t (j e)").unsqueeze(2).to_broadcast(shape)
+                sin_bc = sin_pairs[:].rearrange("p t j e -> p t (j e)").unsqueeze(2).to_broadcast(shape)
+                nc.scalar.copy(out=swapped_pairs[:, :, :, :, 0], in_=pairs[:, :, :, :, 1])
+                nc.scalar.copy(out=swapped_pairs[:, :, :, :, 1], in_=pairs[:, :, :, :, 0])
+                nc.vector.tensor_tensor(out=swapped, in0=swapped, in1=sin_bc, op=MULT)
+                nc.vector.tensor_tensor(out=rotated, in0=rotated, in1=cos_bc, op=MULT)
+                nc.vector.tensor_tensor(out=rotated, in0=rotated, in1=swapped, op=ADD)
+
+                nc.sync.dma_start(
+                    out=out_rows[b].rearrange("(t p) n -> p t n", p=P)[:, :, cols], in_=q[:]
+                )

@@ -40,6 +40,7 @@ def tile_mla_pb_kernel(tc, x, wq_w_words, wq_w_scales, wq_b, cos, sin, out):
         keep = ctx.enter_context(tc.tile_pool(name="keep", bufs=1))
         results = ctx.enter_context(tc.tile_pool(name="results", bufs=BLOCKS * BATCH))
         banks = ctx.enter_context(tc.psum_pool(name="banks", bufs=8))
+        ctx.enter_context(tc.manual_schedule())
 
         x_sb = keep.tile([P, TOKEN_TILES, DIM], BF16)
         x_grouped = keep.tile([P, TOKEN_TILES, PASSES * P * 4], BF16, align_bytes=64)
@@ -56,8 +57,8 @@ def tile_mla_pb_kernel(tc, x, wq_w_words, wq_w_scales, wq_b, cos, sin, out):
         cos_pairs = keep.tile([P, SEQ_TILES, HALF, 2], F32)
         sin_pairs = keep.tile([P, SEQ_TILES, HALF, 2], F32)
 
-        nc.vector.memset(w_scales[:].bitcast(I32), 0)
         nc.vector.memset(bias_rows[:], 0.0)
+        nc.vector.memset(w_scales[:].bitcast(I32), 0)
         make_identity(nc, ident_f32[:])
         make_identity(nc, ident_bf16[:])
 
@@ -124,43 +125,57 @@ def tile_mla_pb_kernel(tc, x, wq_w_words, wq_w_scales, wq_b, cos, sin, out):
                 in_=x_grouped[:, m, :],
             )
 
-        for nb in range(BLOCKS):
+        groups = [(nb, b) for nb in range(BLOCKS) for b in range(BATCH)]
+        q_tiles = {}
+        swapped_tiles = {}
+
+        def rotated_units(nb):
+            return slice((2 - UNITS * nb) % 3, UNITS, 3)
+
+        def multiply_and_swap(nb, b):
             cols = slice(nb * BLOCK, (nb + 1) * BLOCK)
             word_bytes = slice(2 * nb * BLOCK, 2 * (nb + 1) * BLOCK)
-            first = (2 - UNITS * nb) % 3
-            n_rot = len(range(first, UNITS, 3))
-            for b in range(BATCH):
-                q = results.tile([P, SEQ_TILES, BLOCK], F32)
-                for t in range(SEQ_TILES):
-                    m = b * SEQ_TILES + t
-                    acc = banks.tile([P, BLOCK], F32, tag="bank")
-                    for g in range(PASSES):
-                        toks = slice(g * P, (g + 1) * P)
-                        nc.tensor.matmul_mx(
-                            out=acc[:],
-                            lhsT=x_codes[:, m, toks].bitcast(FP8X4),
-                            lhsT_scale=x_scales[:, m, toks],
-                            rhs=w_words[:, g, word_bytes].bitcast(FP4X4),
-                            rhs_scale=w_scales[:, g, cols],
-                            start=(g == 0),
-                            stop=(g == PASSES - 1),
-                        )
-                    nc.vector.tensor_tensor(out=q[:, t, :], in0=acc[:], in1=bias_all[:, cols], op=ADD)
+            q = results.tile([P, SEQ_TILES, BLOCK], F32, name="q")
+            for t in range(SEQ_TILES):
+                m = b * SEQ_TILES + t
+                acc = banks.tile([P, BLOCK], F32, tag="bank")
+                for g in range(PASSES):
+                    toks = slice(g * P, (g + 1) * P)
+                    nc.tensor.matmul_mx(
+                        out=acc[:],
+                        lhsT=x_codes[:, m, toks].bitcast(FP8X4),
+                        lhsT_scale=x_scales[:, m, toks],
+                        rhs=w_words[:, g, word_bytes].bitcast(FP4X4),
+                        rhs_scale=w_scales[:, g, cols],
+                        start=(g == 0),
+                        stop=(g == PASSES - 1),
+                    )
+                nc.vector.tensor_tensor(out=q[:, t, :], in0=acc[:], in1=bias_all[:, cols], op=ADD)
+            pairs = q[:].rearrange("p t (u j e) -> p t u j e", j=HALF, e=2)[:, :, rotated_units(nb), :, :]
+            n_rot = pairs.shape[2]
+            swapped = results.tile([P, SEQ_TILES, MAX_ROT, UNIT], F32, name="swapped")
+            swapped_pairs = swapped[:, :, 0:n_rot, :].rearrange("p t h (j e) -> p t h j e", e=2)
+            nc.scalar.copy(out=swapped_pairs[:, :, :, :, 0], in_=pairs[:, :, :, :, 1])
+            nc.scalar.copy(out=swapped_pairs[:, :, :, :, 1], in_=pairs[:, :, :, :, 0])
+            q_tiles[(nb, b)] = q
+            swapped_tiles[(nb, b)] = swapped
 
-                rotated = q[:].rearrange("p t (u c) -> p t u c", c=UNIT)[:, :, first:UNITS:3, :]
-                pairs = q[:].rearrange("p t (u j e) -> p t u j e", j=HALF, e=2)[:, :, first:UNITS:3, :, :]
-                swapped_full = results.tile([P, SEQ_TILES, MAX_ROT, UNIT], F32)
-                swapped = swapped_full[:, :, 0:n_rot, :]
-                swapped_pairs = swapped.rearrange("p t h (j e) -> p t h j e", e=2)
-                shape = [P, SEQ_TILES, n_rot, UNIT]
-                cos_bc = cos_pairs[:].rearrange("p t j e -> p t (j e)").unsqueeze(2).to_broadcast(shape)
-                sin_bc = sin_pairs[:].rearrange("p t j e -> p t (j e)").unsqueeze(2).to_broadcast(shape)
-                nc.scalar.copy(out=swapped_pairs[:, :, :, :, 0], in_=pairs[:, :, :, :, 1])
-                nc.scalar.copy(out=swapped_pairs[:, :, :, :, 1], in_=pairs[:, :, :, :, 0])
-                nc.vector.tensor_tensor(out=swapped, in0=swapped, in1=sin_bc, op=MULT)
-                nc.vector.tensor_tensor(out=rotated, in0=rotated, in1=cos_bc, op=MULT)
-                nc.vector.tensor_tensor(out=rotated, in0=rotated, in1=swapped, op=ADD)
+        def rotate_and_store(nb, b):
+            cols = slice(nb * BLOCK, (nb + 1) * BLOCK)
+            q = q_tiles[(nb, b)]
+            rotated = q[:].rearrange("p t (u c) -> p t u c", c=UNIT)[:, :, rotated_units(nb), :]
+            n_rot = rotated.shape[2]
+            swapped = swapped_tiles[(nb, b)][:, :, 0:n_rot, :]
+            shape = [P, SEQ_TILES, n_rot, UNIT]
+            cos_bc = cos_pairs[:].rearrange("p t j e -> p t (j e)").unsqueeze(2).to_broadcast(shape)
+            sin_bc = sin_pairs[:].rearrange("p t j e -> p t (j e)").unsqueeze(2).to_broadcast(shape)
+            nc.vector.tensor_tensor(out=swapped, in0=swapped, in1=sin_bc, op=MULT)
+            nc.vector.tensor_tensor(out=rotated, in0=rotated, in1=cos_bc, op=MULT)
+            nc.vector.tensor_tensor(out=rotated, in0=rotated, in1=swapped, op=ADD)
+            nc.sync.dma_start(out=out_rows[b].rearrange("(t p) n -> p t n", p=P)[:, :, cols], in_=q[:])
 
-                nc.sync.dma_start(
-                    out=out_rows[b].rearrange("(t p) n -> p t n", p=P)[:, :, cols], in_=q[:]
-                )
+        for i in range(len(groups)):
+            multiply_and_swap(*groups[i])
+            if i > 0:
+                rotate_and_store(*groups[i - 1])
+        rotate_and_store(*groups[-1])

@@ -82,23 +82,6 @@ def tile_mla_pb_kernel(tc, x, wq_w_words, wq_w_scales, wq_b, cos, sin, out):
                 in_=wq_w_words[:, :, word_bytes].bitcast(I32).rearrange("g p b -> p g b"),
             )
 
-        nc.vector.tensor_copy(
-            out=cos_pairs[:], in_=cos_sb[:].unsqueeze(3).to_broadcast([P, SEQ_TILES, HALF, 2])
-        )
-        nc.vector.tensor_scalar_mul(out=sin_pairs[:, :, :, 0], in0=sin_sb[:], scalar1=-1.0)
-        nc.vector.tensor_copy(out=sin_pairs[:, :, :, 1], in_=sin_sb[:])
-
-        for r in range(BLOCKS):
-            bias_bank = banks.tile([P, BLOCK], F32, tag="bank")
-            nc.tensor.matmul(
-                out=bias_bank[:],
-                lhsT=ident_bf16[:, r : r + 1].to_broadcast([P, P]),
-                rhs=bias_rows[:],
-                start=True,
-                stop=True,
-            )
-            nc.scalar.copy(out=bias_all[:, r * BLOCK : (r + 1) * BLOCK], in_=bias_bank[:])
-
         x_words = x_sb[:].bitcast(F32)
         grouped_words = x_grouped[:].bitcast(F32)
         for m in range(TOKEN_TILES):
@@ -124,6 +107,23 @@ def tile_mla_pb_kernel(tc, x, wq_w_words, wq_w_scales, wq_b, cos, sin, out):
                 scales=x_scales[:, m, :],
                 in_=x_grouped[:, m, :],
             )
+
+        for r in range(BLOCKS):
+            bias_bank = banks.tile([P, BLOCK], F32, tag="bank")
+            nc.tensor.matmul(
+                out=bias_bank[:],
+                lhsT=ident_bf16[:, r : r + 1].to_broadcast([P, P]),
+                rhs=bias_rows[:],
+                start=True,
+                stop=True,
+            )
+            nc.scalar.copy(out=bias_all[:, r * BLOCK : (r + 1) * BLOCK], in_=bias_bank[:])
+
+        nc.vector.tensor_copy(
+            out=cos_pairs[:], in_=cos_sb[:].unsqueeze(3).to_broadcast([P, SEQ_TILES, HALF, 2])
+        )
+        nc.vector.tensor_scalar_mul(out=sin_pairs[:, :, :, 0], in0=sin_sb[:], scalar1=-1.0)
+        nc.vector.tensor_copy(out=sin_pairs[:, :, :, 1], in_=sin_sb[:])
 
         groups = [(nb, b) for nb in range(BLOCKS) for b in range(BATCH)]
         q_tiles = {}
@@ -169,9 +169,9 @@ def tile_mla_pb_kernel(tc, x, wq_w_words, wq_w_scales, wq_b, cos, sin, out):
             shape = [P, SEQ_TILES, n_rot, UNIT]
             cos_bc = cos_pairs[:].rearrange("p t j e -> p t (j e)").unsqueeze(2).to_broadcast(shape)
             sin_bc = sin_pairs[:].rearrange("p t j e -> p t (j e)").unsqueeze(2).to_broadcast(shape)
-            nc.vector.tensor_tensor(out=swapped, in0=swapped, in1=sin_bc, op=MULT)
+            nc.gpsimd.tensor_tensor(out=swapped, in0=swapped, in1=sin_bc, op=MULT)
             nc.vector.tensor_tensor(out=rotated, in0=rotated, in1=cos_bc, op=MULT)
-            nc.vector.tensor_tensor(out=rotated, in0=rotated, in1=swapped, op=ADD)
+            nc.gpsimd.tensor_tensor(out=rotated, in0=rotated, in1=swapped, op=ADD)
             nc.sync.dma_start(out=out_rows[b].rearrange("(t p) n -> p t n", p=P)[:, :, cols], in_=q[:])
 
         for i in range(len(groups)):

@@ -46,8 +46,14 @@ def tile_mla_pb_kernel(tc, x, wq_w_words, wq_w_scales, wq_b, cos, sin, out):
         x_grouped = keep.tile([P, TOKEN_TILES, PASSES * P * 4], BF16, align_bytes=64)
         x_codes = keep.tile([P, TOKEN_TILES, PASSES * P], U32, align_bytes=64)
         x_scales = keep.tile([P, TOKEN_TILES, PASSES * P], U8, align_bytes=64)
-        w_words = keep.tile([P, PASSES, 2 * N_OUT], U8, align_bytes=64)
-        w_scales = keep.tile([P, PASSES, N_OUT], U8, align_bytes=64)
+        w_words = [
+            keep.tile([P, PASSES, 2 * BLOCK], U8, align_bytes=64, name="w_words%d" % nb)
+            for nb in range(BLOCKS)
+        ]
+        w_scales = [
+            keep.tile([P, PASSES, BLOCK], U8, align_bytes=64, name="w_scales%d" % nb)
+            for nb in range(BLOCKS)
+        ]
         bias_rows = keep.tile([P, BLOCK], BF16)
         bias_all = keep.tile([P, N_OUT], F32)
         ident_f32 = keep.tile([P, P], F32)
@@ -58,7 +64,8 @@ def tile_mla_pb_kernel(tc, x, wq_w_words, wq_w_scales, wq_b, cos, sin, out):
         sin_pairs = keep.tile([P, SEQ_TILES, HALF, 2], F32)
 
         nc.vector.memset(bias_rows[:], 0.0)
-        nc.vector.memset(w_scales[:].bitcast(I32), 0)
+        for nb in range(BLOCKS):
+            nc.vector.memset(w_scales[nb][:].bitcast(I32), 0)
         make_identity(nc, ident_f32[:])
         make_identity(nc, ident_bf16[:])
 
@@ -73,12 +80,12 @@ def tile_mla_pb_kernel(tc, x, wq_w_words, wq_w_scales, wq_b, cos, sin, out):
             cols = slice(nb * BLOCK, (nb + 1) * BLOCK)
             for r in range(4):
                 nc.sync.dma_start(
-                    out=w_scales[r:P:32, :, cols].bitcast(I32),
+                    out=w_scales[nb][r:P:32, :, :].bitcast(I32),
                     in_=wq_w_scales[:, r:16:4, cols].bitcast(I32).rearrange("g q n -> q g n"),
                 )
             word_bytes = slice(2 * nb * BLOCK, 2 * (nb + 1) * BLOCK)
             nc.sync.dma_start(
-                out=w_words[:, :, word_bytes].bitcast(I32),
+                out=w_words[nb][:].bitcast(I32),
                 in_=wq_w_words[:, :, word_bytes].bitcast(I32).rearrange("g p b -> p g b"),
             )
 
@@ -134,7 +141,6 @@ def tile_mla_pb_kernel(tc, x, wq_w_words, wq_w_scales, wq_b, cos, sin, out):
 
         def multiply_and_swap(nb, b):
             cols = slice(nb * BLOCK, (nb + 1) * BLOCK)
-            word_bytes = slice(2 * nb * BLOCK, 2 * (nb + 1) * BLOCK)
             q = results.tile([P, SEQ_TILES, BLOCK], F32, name="q")
             for t in range(SEQ_TILES):
                 m = b * SEQ_TILES + t
@@ -145,8 +151,8 @@ def tile_mla_pb_kernel(tc, x, wq_w_words, wq_w_scales, wq_b, cos, sin, out):
                         out=acc[:],
                         lhsT=x_codes[:, m, toks].bitcast(FP8X4),
                         lhsT_scale=x_scales[:, m, toks],
-                        rhs=w_words[:, g, word_bytes].bitcast(FP4X4),
-                        rhs_scale=w_scales[:, g, cols],
+                        rhs=w_words[nb][:, g, :].bitcast(FP4X4),
+                        rhs_scale=w_scales[nb][:, g, :],
                         start=(g == 0),
                         stop=(g == PASSES - 1),
                     )

@@ -35,6 +35,7 @@ def tile_mla_pb_kernel(tc, x, wq_w_words, wq_w_scales, wq_b, cos, sin, out):
     nc = tc.nc
     x_rows = x.flatten_outer_dims()
     out_rows = out.rearrange("b s h d -> b s (h d)")
+    block_order = list(reversed(range(BLOCKS)))
 
     with ExitStack() as ctx:
         keep = ctx.enter_context(tc.tile_pool(name="keep", bufs=1))
@@ -64,7 +65,7 @@ def tile_mla_pb_kernel(tc, x, wq_w_words, wq_w_scales, wq_b, cos, sin, out):
         sin_pairs = keep.tile([P, SEQ_TILES, HALF, 2], F32)
 
         nc.vector.memset(bias_rows[:], 0.0)
-        for nb in range(BLOCKS):
+        for nb in block_order:
             nc.vector.memset(w_scales[nb][:].bitcast(I32), 0)
         make_identity(nc, ident_f32[:])
         make_identity(nc, ident_bf16[:])
@@ -76,7 +77,7 @@ def tile_mla_pb_kernel(tc, x, wq_w_words, wq_w_scales, wq_b, cos, sin, out):
         for m in range(TOKEN_TILES):
             nc.sync.dma_start(out=x_sb[:, m, :], in_=x_rows[m * P : (m + 1) * P, :])
 
-        for nb in range(BLOCKS):
+        for nb in block_order:
             cols = slice(nb * BLOCK, (nb + 1) * BLOCK)
             for r in range(4):
                 nc.sync.dma_start(
@@ -115,7 +116,7 @@ def tile_mla_pb_kernel(tc, x, wq_w_words, wq_w_scales, wq_b, cos, sin, out):
                 in_=x_grouped[:, m, :],
             )
 
-        for r in range(BLOCKS):
+        for r in block_order:
             bias_bank = banks.tile([P, BLOCK], F32, tag="bank")
             nc.tensor.matmul(
                 out=bias_bank[:],
@@ -132,7 +133,7 @@ def tile_mla_pb_kernel(tc, x, wq_w_words, wq_w_scales, wq_b, cos, sin, out):
         nc.vector.tensor_scalar_mul(out=sin_pairs[:, :, :, 0], in0=sin_sb[:], scalar1=-1.0)
         nc.vector.tensor_copy(out=sin_pairs[:, :, :, 1], in_=sin_sb[:])
 
-        groups = [(nb, b) for nb in range(BLOCKS) for b in range(BATCH)]
+        groups = [(nb, b) for nb in block_order for b in range(BATCH)]
         q_tiles = {}
         swapped_tiles = {}
 
@@ -142,6 +143,10 @@ def tile_mla_pb_kernel(tc, x, wq_w_words, wq_w_scales, wq_b, cos, sin, out):
         def multiply_and_swap(nb, b):
             cols = slice(nb * BLOCK, (nb + 1) * BLOCK)
             q = results.tile([P, SEQ_TILES, BLOCK], F32, name="q")
+            swapped = results.tile([P, SEQ_TILES, MAX_ROT, UNIT], F32, name="swapped")
+            pairs = q[:].rearrange("p t (u j e) -> p t u j e", j=HALF, e=2)[:, :, rotated_units(nb), :, :]
+            n_rot = pairs.shape[2]
+            swapped_pairs = swapped[:, :, 0:n_rot, :].rearrange("p t h (j e) -> p t h j e", e=2)
             for t in range(SEQ_TILES):
                 m = b * SEQ_TILES + t
                 acc = banks.tile([P, BLOCK], F32, tag="bank")
@@ -157,12 +162,8 @@ def tile_mla_pb_kernel(tc, x, wq_w_words, wq_w_scales, wq_b, cos, sin, out):
                         stop=(g == PASSES - 1),
                     )
                 nc.vector.tensor_tensor(out=q[:, t, :], in0=acc[:], in1=bias_all[:, cols], op=ADD)
-            pairs = q[:].rearrange("p t (u j e) -> p t u j e", j=HALF, e=2)[:, :, rotated_units(nb), :, :]
-            n_rot = pairs.shape[2]
-            swapped = results.tile([P, SEQ_TILES, MAX_ROT, UNIT], F32, name="swapped")
-            swapped_pairs = swapped[:, :, 0:n_rot, :].rearrange("p t h (j e) -> p t h j e", e=2)
-            nc.scalar.copy(out=swapped_pairs[:, :, :, :, 0], in_=pairs[:, :, :, :, 1])
-            nc.scalar.copy(out=swapped_pairs[:, :, :, :, 1], in_=pairs[:, :, :, :, 0])
+                nc.scalar.copy(out=swapped_pairs[:, t, :, :, 0], in_=pairs[:, t, :, :, 1])
+                nc.scalar.copy(out=swapped_pairs[:, t, :, :, 1], in_=pairs[:, t, :, :, 0])
             q_tiles[(nb, b)] = q
             swapped_tiles[(nb, b)] = swapped
 
@@ -177,8 +178,11 @@ def tile_mla_pb_kernel(tc, x, wq_w_words, wq_w_scales, wq_b, cos, sin, out):
             sin_bc = sin_pairs[:].rearrange("p t j e -> p t (j e)").unsqueeze(2).to_broadcast(shape)
             nc.gpsimd.tensor_tensor(out=swapped, in0=swapped, in1=sin_bc, op=MULT)
             nc.vector.tensor_tensor(out=rotated, in0=rotated, in1=cos_bc, op=MULT)
-            nc.gpsimd.tensor_tensor(out=rotated, in0=rotated, in1=swapped, op=ADD)
-            nc.sync.dma_start(out=out_rows[b].rearrange("(t p) n -> p t n", p=P)[:, :, cols], in_=q[:])
+            nc.gpsimd.tensor_tensor(out=rotated[:, 0, :, :], in0=rotated[:, 0, :, :], in1=swapped[:, 0, :, :], op=ADD)
+            nc.vector.tensor_tensor(out=rotated[:, 1, :, :], in0=rotated[:, 1, :, :], in1=swapped[:, 1, :, :], op=ADD)
+            for t in range(SEQ_TILES):
+                rows = slice(t * P, (t + 1) * P)
+                nc.sync.dma_start(out=out_rows[b, rows, cols], in_=q[:, t, :])
 
         for i in range(len(groups)):
             multiply_and_swap(*groups[i])

@@ -40,7 +40,8 @@ def tile_mla_pb_kernel(tc, x, wq_w_words, wq_w_scales, wq_b, cos, sin, out):
     with ExitStack() as ctx:
         keep = ctx.enter_context(tc.tile_pool(name="keep", bufs=1))
         results = ctx.enter_context(tc.tile_pool(name="results", bufs=BLOCKS * BATCH))
-        banks = ctx.enter_context(tc.psum_pool(name="banks", bufs=8))
+        banks = ctx.enter_context(tc.psum_pool(name="banks", bufs=7))
+        table_banks = ctx.enter_context(tc.psum_pool(name="table_banks", bufs=1))
         ctx.enter_context(tc.manual_schedule())
 
         x_sb = keep.tile([P, TOKEN_TILES, DIM], BF16)
@@ -61,8 +62,7 @@ def tile_mla_pb_kernel(tc, x, wq_w_words, wq_w_scales, wq_b, cos, sin, out):
         ident_bf16 = keep.tile([P, P], BF16)
         cos_sb = keep.tile([P, SEQ_TILES, HALF], BF16)
         sin_sb = keep.tile([P, SEQ_TILES, HALF], BF16)
-        cos_pairs = keep.tile([P, SEQ_TILES, HALF, 2], F32)
-        sin_pairs = keep.tile([P, SEQ_TILES, HALF, 2], F32)
+        tables_bf16 = keep.tile([P, 2, SEQ_TILES, HALF, 2], BF16)
 
         nc.vector.memset(bias_rows[:], 0.0)
         for nb in block_order:
@@ -128,10 +128,18 @@ def tile_mla_pb_kernel(tc, x, wq_w_words, wq_w_scales, wq_b, cos, sin, out):
             nc.scalar.copy(out=bias_all[:, r * BLOCK : (r + 1) * BLOCK], in_=bias_bank[:])
 
         nc.vector.tensor_copy(
-            out=cos_pairs[:], in_=cos_sb[:].unsqueeze(3).to_broadcast([P, SEQ_TILES, HALF, 2])
+            out=tables_bf16[:, 0, :, :, :], in_=cos_sb[:].unsqueeze(3).to_broadcast([P, SEQ_TILES, HALF, 2])
         )
-        nc.vector.tensor_scalar_mul(out=sin_pairs[:, :, :, 0], in0=sin_sb[:], scalar1=-1.0)
-        nc.vector.tensor_copy(out=sin_pairs[:, :, :, 1], in_=sin_sb[:])
+        nc.vector.tensor_scalar_mul(out=tables_bf16[:, 1, :, :, 0], in0=sin_sb[:], scalar1=-1.0)
+        nc.vector.tensor_copy(out=tables_bf16[:, 1, :, :, 1], in_=sin_sb[:])
+        tables = table_banks.tile([P, 2, SEQ_TILES, UNIT], F32)
+        nc.tensor.matmul(
+            out=tables[:].rearrange("p w t c -> p (w t c)"),
+            lhsT=ident_bf16[:],
+            rhs=tables_bf16[:].rearrange("p w t j e -> p (w t j e)"),
+            start=True,
+            stop=True,
+        )
 
         groups = [(nb, b) for nb in block_order for b in range(BATCH)]
         q_tiles = {}
@@ -140,52 +148,62 @@ def tile_mla_pb_kernel(tc, x, wq_w_words, wq_w_scales, wq_b, cos, sin, out):
         def rotated_units(nb):
             return slice((2 - UNITS * nb) % 3, UNITS, 3)
 
-        def multiply_and_swap(nb, b):
+        def multiply(nb, b, t):
             cols = slice(nb * BLOCK, (nb + 1) * BLOCK)
-            q = results.tile([P, SEQ_TILES, BLOCK], F32, name="q")
-            swapped = results.tile([P, SEQ_TILES, MAX_ROT, UNIT], F32, name="swapped")
+            if t == 0:
+                q_new = results.tile([P, SEQ_TILES, BLOCK], F32, name="q")
+                q_tiles[(nb, b)] = q_new
+            q = q_tiles[(nb, b)]
+            m = b * SEQ_TILES + t
+            acc = banks.tile([P, BLOCK], F32, tag="bank")
+            for g in range(PASSES):
+                toks = slice(g * P, (g + 1) * P)
+                nc.tensor.matmul_mx(
+                    out=acc[:],
+                    lhsT=x_codes[:, m, toks].bitcast(FP8X4),
+                    lhsT_scale=x_scales[:, m, toks],
+                    rhs=w_words[nb][:, g, :].bitcast(FP4X4),
+                    rhs_scale=w_scales[nb][:, g, :],
+                    start=(g == 0),
+                    stop=(g == PASSES - 1),
+                )
+            nc.vector.tensor_tensor(out=q[:, t, :], in0=acc[:], in1=bias_all[:, cols], op=ADD)
+
+        def sine_products(nb, b):
+            q = q_tiles[(nb, b)]
             pairs = q[:].rearrange("p t (u j e) -> p t u j e", j=HALF, e=2)[:, :, rotated_units(nb), :, :]
             n_rot = pairs.shape[2]
-            swapped_pairs = swapped[:, :, 0:n_rot, :].rearrange("p t h (j e) -> p t h j e", e=2)
-            for t in range(SEQ_TILES):
-                m = b * SEQ_TILES + t
-                acc = banks.tile([P, BLOCK], F32, tag="bank")
-                for g in range(PASSES):
-                    toks = slice(g * P, (g + 1) * P)
-                    nc.tensor.matmul_mx(
-                        out=acc[:],
-                        lhsT=x_codes[:, m, toks].bitcast(FP8X4),
-                        lhsT_scale=x_scales[:, m, toks],
-                        rhs=w_words[nb][:, g, :].bitcast(FP4X4),
-                        rhs_scale=w_scales[nb][:, g, :],
-                        start=(g == 0),
-                        stop=(g == PASSES - 1),
-                    )
-                nc.vector.tensor_tensor(out=q[:, t, :], in0=acc[:], in1=bias_all[:, cols], op=ADD)
-                nc.scalar.copy(out=swapped_pairs[:, t, :, :, 0], in_=pairs[:, t, :, :, 1])
-                nc.scalar.copy(out=swapped_pairs[:, t, :, :, 1], in_=pairs[:, t, :, :, 0])
-            q_tiles[(nb, b)] = q
+            swapped = results.tile([P, SEQ_TILES, MAX_ROT, UNIT], F32, name="swapped")
             swapped_tiles[(nb, b)] = swapped
+            for t in range(SEQ_TILES):
+                nc.vector.tensor_tensor(
+                    out=swapped[:, t, 0:n_rot, :].rearrange("p u (j e) -> p u j e", e=2),
+                    in0=pairs[:, t, :, :, ::-1],
+                    in1=tables[:, 1, t, :].rearrange("p (j e) -> p j e", e=2).unsqueeze(1).to_broadcast([P, n_rot, HALF, 2]),
+                    op=MULT,
+                )
 
-        def rotate_and_store(nb, b):
+        def cosine_products_sum_store(nb, b):
             cols = slice(nb * BLOCK, (nb + 1) * BLOCK)
             q = q_tiles[(nb, b)]
             rotated = q[:].rearrange("p t (u c) -> p t u c", c=UNIT)[:, :, rotated_units(nb), :]
             n_rot = rotated.shape[2]
             swapped = swapped_tiles[(nb, b)][:, :, 0:n_rot, :]
             shape = [P, SEQ_TILES, n_rot, UNIT]
-            cos_bc = cos_pairs[:].rearrange("p t j e -> p t (j e)").unsqueeze(2).to_broadcast(shape)
-            sin_bc = sin_pairs[:].rearrange("p t j e -> p t (j e)").unsqueeze(2).to_broadcast(shape)
-            nc.gpsimd.tensor_tensor(out=swapped, in0=swapped, in1=sin_bc, op=MULT)
-            nc.vector.tensor_tensor(out=rotated, in0=rotated, in1=cos_bc, op=MULT)
-            nc.gpsimd.tensor_tensor(out=rotated[:, 0, :, :], in0=rotated[:, 0, :, :], in1=swapped[:, 0, :, :], op=ADD)
-            nc.vector.tensor_tensor(out=rotated[:, 1, :, :], in0=rotated[:, 1, :, :], in1=swapped[:, 1, :, :], op=ADD)
+            nc.vector.tensor_tensor(
+                out=rotated, in0=rotated, in1=tables[:, 0, :, :].unsqueeze(2).to_broadcast(shape), op=MULT
+            )
+            nc.gpsimd.tensor_tensor(out=rotated, in0=rotated, in1=swapped, op=ADD)
             for t in range(SEQ_TILES):
                 rows = slice(t * P, (t + 1) * P)
                 nc.sync.dma_start(out=out_rows[b, rows, cols], in_=q[:, t, :])
 
         for i in range(len(groups)):
-            multiply_and_swap(*groups[i])
+            multiply(groups[i][0], groups[i][1], 0)
             if i > 0:
-                rotate_and_store(*groups[i - 1])
-        rotate_and_store(*groups[-1])
+                sine_products(*groups[i - 1])
+            multiply(groups[i][0], groups[i][1], 1)
+            if i > 0:
+                cosine_products_sum_store(*groups[i - 1])
+        sine_products(*groups[-1])
+        cosine_products_sum_store(*groups[-1])

@@ -27,6 +27,7 @@ UNIT = 64
 UNITS = BLOCK // UNIT
 MAX_ROT = 3
 HALF = UNIT // 2
+PIECE = 128
 
 FLOPS = 2 * BATCH * SEQ * DIM * N_OUT
 
@@ -36,6 +37,7 @@ def tile_mla_pb_kernel(tc, x, wq_w_words, wq_w_scales, wq_b, cos, sin, out):
     x_rows = x.flatten_outer_dims()
     out_rows = out.rearrange("b s h d -> b s (h d)")
     block_order = list(reversed(range(BLOCKS)))
+    last_block = block_order[-1]
 
     with ExitStack() as ctx:
         keep = ctx.enter_context(tc.tile_pool(name="keep", bufs=1))
@@ -44,10 +46,16 @@ def tile_mla_pb_kernel(tc, x, wq_w_words, wq_w_scales, wq_b, cos, sin, out):
         table_banks = ctx.enter_context(tc.psum_pool(name="table_banks", bufs=1))
         ctx.enter_context(tc.manual_schedule())
 
-        x_sb = keep.tile([P, TOKEN_TILES, DIM], BF16)
-        x_grouped = keep.tile([P, TOKEN_TILES, PASSES * P * 4], BF16, align_bytes=64)
-        x_codes = keep.tile([P, TOKEN_TILES, PASSES * P], U32, align_bytes=64)
-        x_scales = keep.tile([P, TOKEN_TILES, PASSES * P], U8, align_bytes=64)
+        x_pieces = [2, 1, 1, 1]
+        x_sb = [
+            [keep.tile([P, DIM // x_pieces[m]], BF16, name="x_sb%d_%d" % (m, i)) for i in range(x_pieces[m])]
+            for m in range(TOKEN_TILES)
+        ]
+        x_grouped = [
+            keep.tile([P, PASSES * P * 4], BF16, align_bytes=64, name="x_grouped%d" % m) for m in range(TOKEN_TILES)
+        ]
+        x_codes = [keep.tile([P, PASSES * P], U32, align_bytes=64, name="x_codes%d" % m) for m in range(TOKEN_TILES)]
+        x_scales = [keep.tile([P, PASSES * P], U8, align_bytes=64, name="x_scales%d" % m) for m in range(TOKEN_TILES)]
         w_words = [
             keep.tile([P, PASSES, 2 * BLOCK], U8, align_bytes=64, name="w_words%d" % nb)
             for nb in range(BLOCKS)
@@ -57,25 +65,29 @@ def tile_mla_pb_kernel(tc, x, wq_w_words, wq_w_scales, wq_b, cos, sin, out):
             for nb in range(BLOCKS)
         ]
         bias_rows = keep.tile([P, BLOCK], BF16)
-        bias_all = keep.tile([P, N_OUT], F32)
+        bias_sb = [keep.tile([P, BLOCK], F32, name="bias_sb%d" % nb) for nb in range(BLOCKS)]
         ident_f32 = keep.tile([P, P], F32)
         ident_bf16 = keep.tile([P, P], BF16)
         cos_sb = keep.tile([P, SEQ_TILES, HALF], BF16)
         sin_sb = keep.tile([P, SEQ_TILES, HALF], BF16)
         tables_bf16 = keep.tile([P, 2, SEQ_TILES, HALF, 2], BF16)
+        cos_pairs = keep.tile([P, SEQ_TILES, UNIT], F32)
 
         nc.vector.memset(bias_rows[:], 0.0)
         for nb in block_order:
             nc.vector.memset(w_scales[nb][:].bitcast(I32), 0)
-        make_identity(nc, ident_f32[:])
         make_identity(nc, ident_bf16[:])
+        make_identity(nc, ident_f32[:])
 
-        nc.scalar.dma_start(out=bias_rows[0:BLOCKS, :], in_=wq_b.rearrange("(r c) -> r c", c=BLOCK))
         nc.scalar.dma_start(out=cos_sb[:], in_=cos.rearrange("(t p) j -> p t j", p=P))
         nc.scalar.dma_start(out=sin_sb[:], in_=sin.rearrange("(t p) j -> p t j", p=P))
 
         for m in range(TOKEN_TILES):
-            nc.sync.dma_start(out=x_sb[:, m, :], in_=x_rows[m * P : (m + 1) * P, :])
+            width = DIM // x_pieces[m]
+            for i in range(x_pieces[m]):
+                nc.sync.dma_start(out=x_sb[m][i][:], in_=x_rows[m * P : (m + 1) * P, i * width : (i + 1) * width])
+            if m == 0:
+                nc.sync.dma_start(out=bias_rows[0:BLOCKS, :], in_=wq_b.rearrange("(r c) -> r c", c=BLOCK))
 
         for nb in block_order:
             cols = slice(nb * BLOCK, (nb + 1) * BLOCK)
@@ -90,84 +102,123 @@ def tile_mla_pb_kernel(tc, x, wq_w_words, wq_w_scales, wq_b, cos, sin, out):
                 in_=wq_w_words[:, :, word_bytes].bitcast(I32).rearrange("g p b -> p g b"),
             )
 
-        x_words = x_sb[:].bitcast(F32)
-        grouped_words = x_grouped[:].bitcast(F32)
-        for m in range(TOKEN_TILES):
-            for half in range(PASSES // 2):
-                turned = banks.tile([P, 4, P], F32, tag="bank")
-                for i in range(4):
-                    g, u = 2 * half + i // 2, i % 2
-                    nc.tensor.transpose(
-                        turned[:, i, :],
-                        x_words[:, m, 256 * g + u : 256 * (g + 1) : 2],
-                        ident_f32[:],
-                    )
-                dst = grouped_words[:, m, 512 * half : 512 * (half + 1)].rearrange(
-                    "p (g r u) -> p g r u", g=2, u=2
-                )
-                src = turned[:].rearrange("p (g u) r -> p g r u", u=2)
-                if half == 0:
-                    nc.vector.tensor_copy(out=dst, in_=src)
-                else:
-                    nc.scalar.copy(out=dst, in_=src)
-            nc.vector.quantize_mx(
-                out=x_codes[:, m, :].bitcast(FP8X4),
-                scales=x_scales[:, m, :],
-                in_=x_grouped[:, m, :],
-            )
-
-        for r in block_order:
-            bias_bank = banks.tile([P, BLOCK], F32, tag="bank")
-            nc.tensor.matmul(
-                out=bias_bank[:],
-                lhsT=ident_bf16[:, r : r + 1].to_broadcast([P, P]),
-                rhs=bias_rows[:],
-                start=True,
-                stop=True,
-            )
-            nc.scalar.copy(out=bias_all[:, r * BLOCK : (r + 1) * BLOCK], in_=bias_bank[:])
-
         nc.vector.tensor_copy(
             out=tables_bf16[:, 0, :, :, :], in_=cos_sb[:].unsqueeze(3).to_broadcast([P, SEQ_TILES, HALF, 2])
         )
         nc.vector.tensor_scalar_mul(out=tables_bf16[:, 1, :, :, 0], in0=sin_sb[:], scalar1=-1.0)
         nc.vector.tensor_copy(out=tables_bf16[:, 1, :, :, 1], in_=sin_sb[:])
-        tables = table_banks.tile([P, 2, SEQ_TILES, UNIT], F32)
-        nc.tensor.matmul(
-            out=tables[:].rearrange("p w t c -> p (w t c)"),
-            lhsT=ident_bf16[:],
-            rhs=tables_bf16[:].rearrange("p w t j e -> p (w t j e)"),
-            start=True,
-            stop=True,
+        nc.vector.tensor_copy(
+            out=cos_pairs[:].rearrange("p t (j e) -> p t j e", e=2),
+            in_=cos_sb[:].unsqueeze(3).to_broadcast([P, SEQ_TILES, HALF, 2]),
         )
+        tables = table_banks.tile([P, 2, SEQ_TILES, UNIT], F32)
 
-        groups = [(nb, b) for nb in block_order for b in range(BATCH)]
+        def tables_to_psum():
+            nc.tensor.matmul(
+                out=tables[:].rearrange("p w t c -> p (w t c)"),
+                lhsT=ident_bf16[:],
+                rhs=tables_bf16[:].rearrange("p w t j e -> p (w t j e)"),
+                start=True,
+                stop=True,
+            )
+
+        def spread_bias(nb):
+            bias_bank = banks.tile([P, BLOCK], F32, tag="bank")
+            nc.tensor.matmul(
+                out=bias_bank[:],
+                lhsT=ident_bf16[:, nb : nb + 1].to_broadcast([P, P]),
+                rhs=bias_rows[:],
+                start=True,
+                stop=True,
+            )
+            nc.scalar.copy(out=bias_sb[nb][:], in_=bias_bank[:])
+
+        def turn(m):
+            passes_in_piece = PASSES // x_pieces[m]
+            grouped_words = x_grouped[m][:].bitcast(F32)
+            for half in range(PASSES // 2):
+                turned = banks.tile([P, 4, P], F32, tag="bank")
+                for i in range(4):
+                    g, u = 2 * half + i // 2, i % 2
+                    words = x_sb[m][g // passes_in_piece][:].bitcast(F32)
+                    first = 256 * (g % passes_in_piece)
+                    nc.tensor.transpose(turned[:, i, :], words[:, first + u : first + 256 : 2], ident_f32[:])
+                dst = grouped_words[:, 512 * half : 512 * (half + 1)].rearrange("p (g r u) -> p g r u", g=2, u=2)
+                src = turned[:].rearrange("p (g u) r -> p g r u", u=2)
+                if half == 0:
+                    nc.vector.tensor_copy(out=dst, in_=src)
+                else:
+                    nc.scalar.copy(out=dst, in_=src)
+
+        def quantise(m):
+            nc.vector.quantize_mx(out=x_codes[m][:].bitcast(FP8X4), scales=x_scales[m][:], in_=x_grouped[m][:])
+
+        turn(0)
+        tables_to_psum()
+        spread_bias(block_order[0])
+        spread_bias(block_order[1])
+        turn(1)
+        quantise(0)
+        spread_bias(block_order[2])
+        spread_bias(block_order[3])
+        turn(2)
+        quantise(1)
+        spread_bias(block_order[4])
+        turn(3)
+        quantise(2)
+        spread_bias(block_order[5])
+        quantise(3)
+
         q_tiles = {}
         swapped_tiles = {}
 
         def rotated_units(nb):
             return slice((2 - UNITS * nb) % 3, UNITS, 3)
 
-        def multiply(nb, b, t):
-            cols = slice(nb * BLOCK, (nb + 1) * BLOCK)
-            if t == 0:
-                q_new = results.tile([P, SEQ_TILES, BLOCK], F32, name="q")
-                q_tiles[(nb, b)] = q_new
-            q = q_tiles[(nb, b)]
-            m = b * SEQ_TILES + t
-            acc = banks.tile([P, BLOCK], F32, tag="bank")
+        def multiply(acc, nb, m, first, width):
             for g in range(PASSES):
                 toks = slice(g * P, (g + 1) * P)
                 nc.tensor.matmul_mx(
-                    out=acc[:],
-                    lhsT=x_codes[:, m, toks].bitcast(FP8X4),
-                    lhsT_scale=x_scales[:, m, toks],
-                    rhs=w_words[nb][:, g, :].bitcast(FP4X4),
-                    rhs_scale=w_scales[nb][:, g, :],
+                    out=acc,
+                    lhsT=x_codes[m][:, toks].bitcast(FP8X4),
+                    lhsT_scale=x_scales[m][:, toks],
+                    rhs=w_words[nb][:, g, 2 * first : 2 * (first + width)].bitcast(FP4X4),
+                    rhs_scale=w_scales[nb][:, g, first : first + width],
                     start=(g == 0),
                     stop=(g == PASSES - 1),
                 )
-            nc.vector.tensor_tensor(out=q[:, t, :], in0=acc[:], in1=bias_all[:, cols], op=ADD)
+
+        def result_tile(nb, m):
+            b = m // SEQ_TILES
+            if (nb, b) not in q_tiles:
+                q_new = results.tile([P, SEQ_TILES, BLOCK], F32, name="q")
+                q_tiles[(nb, b)] = q_new
+            return q_tiles[(nb, b)][:, m % SEQ_TILES, :]
+
+        def whole_block(nb, m):
+            acc = banks.tile([P, BLOCK], F32, tag="bank")
+            multiply(acc[:], nb, m, 0, BLOCK)
+            nc.vector.tensor_tensor(out=result_tile(nb, m), in0=acc[:], in1=bias_sb[nb][:], op=ADD)
+
+        def two_pieces(nb, m, pieces):
+            acc = banks.tile([P, 2, PIECE], F32, tag="bank")
+            for i in range(2):
+                multiply(acc[:, i, :], nb, m, (pieces.start + i * pieces.step) * PIECE, PIECE)
+            nc.vector.tensor_tensor(
+                out=result_tile(nb, m).rearrange("p (s c) -> p s c", c=PIECE)[:, pieces, :],
+                in0=acc[:],
+                in1=bias_sb[nb][:].rearrange("p (s c) -> p s c", c=PIECE)[:, pieces, :],
+                op=ADD,
+            )
+
+        def store_pieces(queue, nb, m, pieces):
+            b, t = m // SEQ_TILES, m % SEQ_TILES
+            queue.dma_start(
+                out=out_rows[b, t * P : (t + 1) * P, nb * BLOCK : (nb + 1) * BLOCK].rearrange(
+                    "r (s c) -> r s c", c=PIECE
+                )[:, pieces, :],
+                in_=result_tile(nb, m).rearrange("p (s c) -> p s c", c=PIECE)[:, pieces, :],
+            )
 
         def sine_products(nb, b):
             q = q_tiles[(nb, b)]
@@ -183,27 +234,56 @@ def tile_mla_pb_kernel(tc, x, wq_w_words, wq_w_scales, wq_b, cos, sin, out):
                     op=MULT,
                 )
 
-        def cosine_products_sum_store(nb, b):
-            cols = slice(nb * BLOCK, (nb + 1) * BLOCK)
+        def cosine_products_and_sum(nb, b, on_gpsimd):
             q = q_tiles[(nb, b)]
             rotated = q[:].rearrange("p t (u c) -> p t u c", c=UNIT)[:, :, rotated_units(nb), :]
             n_rot = rotated.shape[2]
             swapped = swapped_tiles[(nb, b)][:, :, 0:n_rot, :]
+            straight_tile = results.tile([P, SEQ_TILES, MAX_ROT, UNIT], F32, name="straight")
+            straight = straight_tile[:, :, 0:n_rot, :]
             shape = [P, SEQ_TILES, n_rot, UNIT]
-            nc.vector.tensor_tensor(
-                out=rotated, in0=rotated, in1=tables[:, 0, :, :].unsqueeze(2).to_broadcast(shape), op=MULT
-            )
-            nc.gpsimd.tensor_tensor(out=rotated, in0=rotated, in1=swapped, op=ADD)
-            for t in range(SEQ_TILES):
-                rows = slice(t * P, (t + 1) * P)
-                nc.sync.dma_start(out=out_rows[b, rows, cols], in_=q[:, t, :])
+            if on_gpsimd:
+                nc.gpsimd.tensor_tensor(
+                    out=straight, in0=rotated, in1=cos_pairs[:].unsqueeze(2).to_broadcast(shape), op=MULT
+                )
+            else:
+                nc.vector.tensor_tensor(
+                    out=straight, in0=rotated, in1=tables[:, 0, :, :].unsqueeze(2).to_broadcast(shape), op=MULT
+                )
+            nc.gpsimd.tensor_tensor(out=rotated, in0=straight, in1=swapped, op=ADD)
 
-        for i in range(len(groups)):
-            multiply(groups[i][0], groups[i][1], 0)
-            if i > 0:
-                sine_products(*groups[i - 1])
-            multiply(groups[i][0], groups[i][1], 1)
-            if i > 0:
-                cosine_products_sum_store(*groups[i - 1])
-        sine_products(*groups[-1])
-        cosine_products_sum_store(*groups[-1])
+        middle = slice(1, 3, 1)
+        outer = slice(0, 4, 3)
+        jobs = [(nb, m, None) for nb in block_order[:-1] for m in range(TOKEN_TILES)]
+        jobs.extend([(last_block, m, middle) for m in range(TOKEN_TILES)])
+        jobs.extend([(last_block, m, outer) for m in range(TOKEN_TILES)])
+        due = []
+        done = 0
+        n_groups = 0
+        for nb, m, pieces in jobs:
+            b = m // SEQ_TILES
+            if pieces is None:
+                whole_block(nb, m)
+            else:
+                two_pieces(nb, m, pieces)
+                if pieces == outer:
+                    store_pieces(nc.scalar, nb, m, outer)
+            if done < len(due):
+                step, s_nb, s_b, s_n = due[done]
+                done += 1
+                if step == 0:
+                    sine_products(s_nb, s_b)
+                else:
+                    cosine_products_and_sum(s_nb, s_b, s_n % 2 == 0)
+                    for t in range(SEQ_TILES):
+                        if s_nb == last_block:
+                            store_pieces(nc.sync, s_nb, s_b * SEQ_TILES + t, middle)
+                        else:
+                            nc.sync.dma_start(
+                                out=out_rows[s_b, t * P : (t + 1) * P, s_nb * BLOCK : (s_nb + 1) * BLOCK],
+                                in_=q_tiles[(s_nb, s_b)][:, t, :],
+                            )
+            if m % SEQ_TILES == SEQ_TILES - 1 and pieces != outer:
+                due.extend([(0, nb, b, n_groups), (1, nb, b, n_groups)])
+                n_groups += 1
+        assert done == len(due)

@@ -274,7 +274,7 @@ def tile_mla_pb_kernel(tc, x, wq_w_words, wq_w_scales, wq_b, cos, sin, out):
                 if step == 0:
                     sine_products(s_nb, s_b)
                 else:
-                    cosine_products_and_sum(s_nb, s_b, s_n % 2 == 0)
+                    cosine_products_and_sum(s_nb, s_b, False)
                     for t in range(SEQ_TILES):
                         if s_nb == last_block:
                             store_pieces(nc.sync, s_nb, s_b * SEQ_TILES + t, middle)

@@ -46,7 +46,7 @@ def tile_mla_pb_kernel(tc, x, wq_w_words, wq_w_scales, wq_b, cos, sin, out):
         table_banks = ctx.enter_context(tc.psum_pool(name="table_banks", bufs=1))
         ctx.enter_context(tc.manual_schedule())
 
-        x_pieces = [2, 1, 1, 1]
+        x_pieces = [4, 1, 1, 1]
         x_sb = [
             [keep.tile([P, DIM // x_pieces[m]], BF16, name="x_sb%d_%d" % (m, i)) for i in range(x_pieces[m])]
             for m in range(TOKEN_TILES)
@@ -154,19 +154,15 @@ def tile_mla_pb_kernel(tc, x, wq_w_words, wq_w_scales, wq_b, cos, sin, out):
             nc.vector.quantize_mx(out=x_codes[m][:].bitcast(FP8X4), scales=x_scales[m][:], in_=x_grouped[m][:])
 
         turn(0)
-        tables_to_psum()
-        spread_bias(block_order[0])
-        spread_bias(block_order[1])
         turn(1)
         quantise(0)
-        spread_bias(block_order[2])
-        spread_bias(block_order[3])
+        tables_to_psum()
+        for nb in block_order:
+            spread_bias(nb)
         turn(2)
         quantise(1)
-        spread_bias(block_order[4])
         turn(3)
         quantise(2)
-        spread_bias(block_order[5])
         quantise(3)
 
         q_tiles = {}

@@ -36,8 +36,9 @@ def tile_mla_pb_kernel(tc, x, wq_w_words, wq_w_scales, wq_b, cos, sin, out):
     nc = tc.nc
     x_rows = x.flatten_outer_dims()
     out_rows = out.rearrange("b s h d -> b s (h d)")
-    block_order = list(reversed(range(BLOCKS)))
-    last_block = block_order[-1]
+    split_blocks = [3, 0]
+    whole_blocks = [5, 4, 2, 1]
+    block_order = whole_blocks + split_blocks
 
     with ExitStack() as ctx:
         keep = ctx.enter_context(tc.tile_pool(name="keep", bufs=1))
@@ -250,9 +251,9 @@ def tile_mla_pb_kernel(tc, x, wq_w_words, wq_w_scales, wq_b, cos, sin, out):
 
         middle = slice(1, 3, 1)
         outer = slice(0, 4, 3)
-        jobs = [(nb, m, None) for nb in block_order[:-1] for m in range(TOKEN_TILES)]
-        jobs.extend([(last_block, m, middle) for m in range(TOKEN_TILES)])
-        jobs.extend([(last_block, m, outer) for m in range(TOKEN_TILES)])
+        jobs = [(nb, m, None) for nb in whole_blocks for m in range(TOKEN_TILES)]
+        jobs.extend([(nb, m, middle) for nb in split_blocks for m in range(TOKEN_TILES)])
+        jobs.extend([(nb, m, outer) for nb in split_blocks for m in range(TOKEN_TILES)])
         due = []
         done = 0
         n_groups = 0
@@ -272,7 +273,7 @@ def tile_mla_pb_kernel(tc, x, wq_w_words, wq_w_scales, wq_b, cos, sin, out):
                 else:
                     cosine_products_and_sum(s_nb, s_b, False)
                     for t in range(SEQ_TILES):
-                        if s_nb == last_block:
+                        if s_nb in split_blocks:
                             store_pieces(nc.sync, s_nb, s_b * SEQ_TILES + t, middle)
                         else:
                             nc.sync.dma_start(

@@ -36,13 +36,13 @@ def tile_mla_pb_kernel(tc, x, wq_w_words, wq_w_scales, wq_b, cos, sin, out):
     nc = tc.nc
     x_rows = x.flatten_outer_dims()
     out_rows = out.rearrange("b s h d -> b s (h d)")
-    split_blocks = [3, 0]
-    whole_blocks = [5, 4, 2, 1]
-    block_order = whole_blocks + split_blocks
+    block_order = [5, 4, 2, 1, 3, 0]
+    last_block = block_order[-1]
+    split_tiles = [2, 3]
 
     with ExitStack() as ctx:
         keep = ctx.enter_context(tc.tile_pool(name="keep", bufs=1))
-        results = ctx.enter_context(tc.tile_pool(name="results", bufs=BLOCKS * BATCH))
+        results = ctx.enter_context(tc.tile_pool(name="results", bufs=BLOCKS * TOKEN_TILES))
         banks = ctx.enter_context(tc.psum_pool(name="banks", bufs=7))
         table_banks = ctx.enter_context(tc.psum_pool(name="table_banks", bufs=1))
         ctx.enter_context(tc.manual_schedule())
@@ -72,7 +72,6 @@ def tile_mla_pb_kernel(tc, x, wq_w_words, wq_w_scales, wq_b, cos, sin, out):
         cos_sb = keep.tile([P, SEQ_TILES, HALF], BF16)
         sin_sb = keep.tile([P, SEQ_TILES, HALF], BF16)
         tables_bf16 = keep.tile([P, 2, SEQ_TILES, HALF, 2], BF16)
-        cos_pairs = keep.tile([P, SEQ_TILES, UNIT], F32)
 
         nc.vector.memset(bias_rows[:], 0.0)
         for nb in block_order:
@@ -106,12 +105,8 @@ def tile_mla_pb_kernel(tc, x, wq_w_words, wq_w_scales, wq_b, cos, sin, out):
         nc.vector.tensor_copy(
             out=tables_bf16[:, 0, :, :, :], in_=cos_sb[:].unsqueeze(3).to_broadcast([P, SEQ_TILES, HALF, 2])
         )
-        nc.vector.tensor_scalar_mul(out=tables_bf16[:, 1, :, :, 0], in0=sin_sb[:], scalar1=-1.0)
-        nc.vector.tensor_copy(out=tables_bf16[:, 1, :, :, 1], in_=sin_sb[:])
-        nc.vector.tensor_copy(
-            out=cos_pairs[:].rearrange("p t (j e) -> p t j e", e=2),
-            in_=cos_sb[:].unsqueeze(3).to_broadcast([P, SEQ_TILES, HALF, 2]),
-        )
+        nc.vector.tensor_copy(out=tables_bf16[:, 1, :, :, 0], in_=sin_sb[:])
+        nc.vector.tensor_scalar_mul(out=tables_bf16[:, 1, :, :, 1], in0=sin_sb[:], scalar1=-1.0)
         tables = table_banks.tile([P, 2, SEQ_TILES, UNIT], F32)
 
         def tables_to_psum():
@@ -158,7 +153,7 @@ def tile_mla_pb_kernel(tc, x, wq_w_words, wq_w_scales, wq_b, cos, sin, out):
         turn(1)
         quantise(0)
         tables_to_psum()
-        for nb in block_order:
+        for nb in block_order[:2]:
             spread_bias(nb)
         turn(2)
         quantise(1)
@@ -167,7 +162,6 @@ def tile_mla_pb_kernel(tc, x, wq_w_words, wq_w_scales, wq_b, cos, sin, out):
         quantise(3)
 
         q_tiles = {}
-        swapped_tiles = {}
 
         def rotated_units(nb):
             return slice((2 - UNITS * nb) % 3, UNITS, 3)
@@ -185,26 +179,28 @@ def tile_mla_pb_kernel(tc, x, wq_w_words, wq_w_scales, wq_b, cos, sin, out):
                     stop=(g == PASSES - 1),
                 )
 
-        def result_tile(nb, m):
-            b = m // SEQ_TILES
-            if (nb, b) not in q_tiles:
-                q_new = results.tile([P, SEQ_TILES, BLOCK], F32, name="q")
-                q_tiles[(nb, b)] = q_new
-            return q_tiles[(nb, b)][:, m % SEQ_TILES, :]
+        def result_tile(nb, m, pieces):
+            if (nb, m, pieces) not in q_tiles:
+                q_new = results.tile([P, BLOCK], F32, name="q")
+                q_tiles[(nb, m, pieces)] = q_new
+            return q_tiles[(nb, m, pieces)][:, 0 : BLOCK if pieces is None else 2 * PIECE]
 
         def whole_block(nb, m):
             acc = banks.tile([P, BLOCK], F32, tag="bank")
             multiply(acc[:], nb, m, 0, BLOCK)
-            nc.vector.tensor_tensor(out=result_tile(nb, m), in0=acc[:], in1=bias_sb[nb][:], op=ADD)
+            nc.vector.tensor_tensor(out=result_tile(nb, m, None), in0=acc[:], in1=bias_sb[nb][:], op=ADD)
+
+        def both(pieces):
+            return slice(pieces[0], pieces[1] + 1, pieces[1] - pieces[0])
 
         def two_pieces(nb, m, pieces):
             acc = banks.tile([P, 2, PIECE], F32, tag="bank")
             for i in range(2):
-                multiply(acc[:, i, :], nb, m, (pieces.start + i * pieces.step) * PIECE, PIECE)
+                multiply(acc[:, i, :], nb, m, pieces[i] * PIECE, PIECE)
             nc.vector.tensor_tensor(
-                out=result_tile(nb, m).rearrange("p (s c) -> p s c", c=PIECE)[:, pieces, :],
+                out=result_tile(nb, m, pieces).rearrange("p (s c) -> p s c", c=PIECE),
                 in0=acc[:],
-                in1=bias_sb[nb][:].rearrange("p (s c) -> p s c", c=PIECE)[:, pieces, :],
+                in1=bias_sb[nb][:].rearrange("p (s c) -> p s c", c=PIECE)[:, both(pieces), :],
                 op=ADD,
             )
 
@@ -213,74 +209,66 @@ def tile_mla_pb_kernel(tc, x, wq_w_words, wq_w_scales, wq_b, cos, sin, out):
             queue.dma_start(
                 out=out_rows[b, t * P : (t + 1) * P, nb * BLOCK : (nb + 1) * BLOCK].rearrange(
                     "r (s c) -> r s c", c=PIECE
-                )[:, pieces, :],
-                in_=result_tile(nb, m).rearrange("p (s c) -> p s c", c=PIECE)[:, pieces, :],
+                )[:, both(pieces), :],
+                in_=result_tile(nb, m, pieces).rearrange("p (s c) -> p s c", c=PIECE),
             )
 
-        def sine_products(nb, b):
-            q = q_tiles[(nb, b)]
-            pairs = q[:].rearrange("p t (u j e) -> p t u j e", j=HALF, e=2)[:, :, rotated_units(nb), :, :]
-            n_rot = pairs.shape[2]
-            swapped = results.tile([P, SEQ_TILES, MAX_ROT, UNIT], F32, name="swapped")
-            swapped_tiles[(nb, b)] = swapped
-            for t in range(SEQ_TILES):
-                nc.vector.tensor_tensor(
-                    out=swapped[:, t, 0:n_rot, :].rearrange("p u (j e) -> p u j e", e=2),
-                    in0=pairs[:, t, :, :, ::-1],
-                    in1=tables[:, 1, t, :].rearrange("p (j e) -> p j e", e=2).unsqueeze(1).to_broadcast([P, n_rot, HALF, 2]),
-                    op=MULT,
-                )
+        def rotate(nb, m, pieces):
+            units = result_tile(nb, m, pieces).rearrange("p (u c) -> p u c", c=UNIT)
+            rotated = units[:, rotated_units(nb) if pieces is None else slice(0, 4, 3), :]
+            n_rot = rotated.shape[1]
+            shape = [P, 2, n_rot, UNIT]
+            products_tile = results.tile([P, 2, MAX_ROT, UNIT], F32, name="products")
+            products = products_tile[:, :, 0:n_rot, :]
+            nc.vector.tensor_tensor(
+                out=products,
+                in0=rotated.unsqueeze(1).to_broadcast(shape),
+                in1=tables[:, :, m % SEQ_TILES, :].unsqueeze(2).to_broadcast(shape),
+                op=MULT,
+            )
+            nc.gpsimd.tensor_tensor(
+                out=rotated.rearrange("p u (j e) -> p u j e", e=2),
+                in0=products[:, 0, :, :].rearrange("p u (j e) -> p u j e", e=2),
+                in1=products[:, 1, :, :].rearrange("p u (j e) -> p u j e", e=2)[:, :, :, ::-1],
+                op=ADD,
+            )
 
-        def cosine_products_and_sum(nb, b, on_gpsimd):
-            q = q_tiles[(nb, b)]
-            rotated = q[:].rearrange("p t (u c) -> p t u c", c=UNIT)[:, :, rotated_units(nb), :]
-            n_rot = rotated.shape[2]
-            swapped = swapped_tiles[(nb, b)][:, :, 0:n_rot, :]
-            straight_tile = results.tile([P, SEQ_TILES, MAX_ROT, UNIT], F32, name="straight")
-            straight = straight_tile[:, :, 0:n_rot, :]
-            shape = [P, SEQ_TILES, n_rot, UNIT]
-            if on_gpsimd:
-                nc.gpsimd.tensor_tensor(
-                    out=straight, in0=rotated, in1=cos_pairs[:].unsqueeze(2).to_broadcast(shape), op=MULT
+        middle = (1, 2)
+        outer = (0, 3)
+        jobs = [(nb, m, None) for nb in block_order for m in range(TOKEN_TILES)]
+        jobs = jobs[: -len(split_tiles)]
+        jobs.extend([(last_block, m, middle) for m in split_tiles])
+        jobs.extend([(last_block, m, outer) for m in split_tiles])
+        due = []
+
+        def rotate_next():
+            nb, m, pieces = due[0]
+            due.remove(due[0])
+            rotate(nb, m, pieces)
+            if pieces is None:
+                b, t = m // SEQ_TILES, m % SEQ_TILES
+                nc.sync.dma_start(
+                    out=out_rows[b, t * P : (t + 1) * P, nb * BLOCK : (nb + 1) * BLOCK],
+                    in_=result_tile(nb, m, None)
                 )
             else:
-                nc.vector.tensor_tensor(
-                    out=straight, in0=rotated, in1=tables[:, 0, :, :].unsqueeze(2).to_broadcast(shape), op=MULT
-                )
-            nc.gpsimd.tensor_tensor(out=rotated, in0=straight, in1=swapped, op=ADD)
+                store_pieces(nc.sync, nb, m, pieces)
 
-        middle = slice(1, 3, 1)
-        outer = slice(0, 4, 3)
-        jobs = [(nb, m, None) for nb in whole_blocks for m in range(TOKEN_TILES)]
-        jobs.extend([(nb, m, middle) for nb in split_blocks for m in range(TOKEN_TILES)])
-        jobs.extend([(nb, m, outer) for nb in split_blocks for m in range(TOKEN_TILES)])
-        due = []
-        done = 0
-        n_groups = 0
-        for nb, m, pieces in jobs:
-            b = m // SEQ_TILES
+        for job in jobs:
+            nb, m, pieces = job
+            ahead = block_order.index(nb) + 2
+            if m == 1 and pieces is None and ahead < BLOCKS:
+                spread_bias(block_order[ahead])
+            if pieces == outer:
+                while len(due) > 0:
+                    rotate_next()
             if pieces is None:
                 whole_block(nb, m)
             else:
                 two_pieces(nb, m, pieces)
-                if pieces == outer:
-                    store_pieces(nc.scalar, nb, m, outer)
-            if done < len(due):
-                step, s_nb, s_b, s_n = due[done]
-                done += 1
-                if step == 0:
-                    sine_products(s_nb, s_b)
-                else:
-                    cosine_products_and_sum(s_nb, s_b, False)
-                    for t in range(SEQ_TILES):
-                        if s_nb in split_blocks:
-                            store_pieces(nc.sync, s_nb, s_b * SEQ_TILES + t, middle)
-                        else:
-                            nc.sync.dma_start(
-                                out=out_rows[s_b, t * P : (t + 1) * P, s_nb * BLOCK : (s_nb + 1) * BLOCK],
-                                in_=q_tiles[(s_nb, s_b)][:, t, :],
-                            )
-            if m % SEQ_TILES == SEQ_TILES - 1 and pieces != outer:
-                due.extend([(0, nb, b, n_groups), (1, nb, b, n_groups)])
-                n_groups += 1
-        assert done == len(due)
+            if pieces == outer:
+                store_pieces(nc.scalar, nb, m, outer)
+                continue
+            if len(due) > 0:
+                rotate_next()
+            due.extend([job])

@@ -47,7 +47,7 @@ def tile_mla_pb_kernel(tc, x, wq_w_words, wq_w_scales, wq_b, cos, sin, out):
         table_banks = ctx.enter_context(tc.psum_pool(name="table_banks", bufs=1))
         ctx.enter_context(tc.manual_schedule())
 
-        x_pieces = [4, 1, 1, 1]
+        x_pieces = [2, 1, 1, 1]
         x_sb = [
             [keep.tile([P, DIM // x_pieces[m]], BF16, name="x_sb%d_%d" % (m, i)) for i in range(x_pieces[m])]
             for m in range(TOKEN_TILES)
@@ -65,7 +65,7 @@ def tile_mla_pb_kernel(tc, x, wq_w_words, wq_w_scales, wq_b, cos, sin, out):
             keep.tile([P, PASSES, BLOCK], U8, align_bytes=64, name="w_scales%d" % nb)
             for nb in range(BLOCKS)
         ]
-        bias_rows = keep.tile([P, BLOCK], BF16)
+        bias_rows = keep.tile([P, N_OUT // 2], BF16)
         bias_sb = [keep.tile([P, BLOCK], F32, name="bias_sb%d" % nb) for nb in range(BLOCKS)]
         ident_f32 = keep.tile([P, P], F32)
         ident_bf16 = keep.tile([P, P], BF16)
@@ -73,40 +73,57 @@ def tile_mla_pb_kernel(tc, x, wq_w_words, wq_w_scales, wq_b, cos, sin, out):
         sin_sb = keep.tile([P, SEQ_TILES, HALF], BF16)
         tables_bf16 = keep.tile([P, 2, SEQ_TILES, HALF, 2], BF16)
 
-        nc.vector.memset(bias_rows[:], 0.0)
-        for nb in block_order:
-            nc.vector.memset(w_scales[nb][:].bitcast(I32), 0)
-        make_identity(nc, ident_bf16[:])
+        def zero_scales(engine, nb):
+            engine.memset(w_scales[nb][:].bitcast(F32), 0.0)
+
+        zero_scales(nc.vector, block_order[0])
+        nc.vector.memset(bias_rows[:].bitcast(I32), 0)
+        zero_scales(nc.vector, block_order[1])
         make_identity(nc, ident_f32[:])
+        make_identity(nc, ident_bf16[:])
+        for nb in block_order[2:]:
+            zero_scales(nc.gpsimd, nb)
 
-        nc.scalar.dma_start(out=cos_sb[:], in_=cos.rearrange("(t p) j -> p t j", p=P))
-        nc.scalar.dma_start(out=sin_sb[:], in_=sin.rearrange("(t p) j -> p t j", p=P))
-
-        for m in range(TOKEN_TILES):
+        def load_x(m):
             width = DIM // x_pieces[m]
             for i in range(x_pieces[m]):
                 nc.sync.dma_start(out=x_sb[m][i][:], in_=x_rows[m * P : (m + 1) * P, i * width : (i + 1) * width])
-            if m == 0:
-                nc.sync.dma_start(out=bias_rows[0:BLOCKS, :], in_=wq_b.rearrange("(r c) -> r c", c=BLOCK))
 
-        for nb in block_order:
+        def load_scales(nb):
             cols = slice(nb * BLOCK, (nb + 1) * BLOCK)
             for r in range(4):
                 nc.sync.dma_start(
                     out=w_scales[nb][r:P:32, :, :].bitcast(I32),
                     in_=wq_w_scales[:, r:16:4, cols].bitcast(I32).rearrange("g q n -> q g n"),
                 )
+
+        def load_words(nb):
             word_bytes = slice(2 * nb * BLOCK, 2 * (nb + 1) * BLOCK)
             nc.sync.dma_start(
                 out=w_words[nb][:].bitcast(I32),
                 in_=wq_w_words[:, :, word_bytes].bitcast(I32).rearrange("g p b -> p g b"),
             )
 
-        nc.vector.tensor_copy(
-            out=tables_bf16[:, 0, :, :, :], in_=cos_sb[:].unsqueeze(3).to_broadcast([P, SEQ_TILES, HALF, 2])
-        )
-        nc.vector.tensor_copy(out=tables_bf16[:, 1, :, :, 0], in_=sin_sb[:])
-        nc.vector.tensor_scalar_mul(out=tables_bf16[:, 1, :, :, 1], in0=sin_sb[:], scalar1=-1.0)
+        load_x(0)
+        nc.sync.dma_start(out=bias_rows[0:2, :], in_=wq_b.rearrange("(r c) -> r c", r=2))
+        load_scales(block_order[0])
+        load_x(1)
+        load_words(block_order[0])
+        load_x(2)
+        load_x(3)
+        nc.sync.dma_start(out=cos_sb[:], in_=cos.rearrange("(t p) j -> p t j", p=P))
+        nc.sync.dma_start(out=sin_sb[:], in_=sin.rearrange("(t p) j -> p t j", p=P))
+        for nb in block_order[1:]:
+            load_scales(nb)
+            load_words(nb)
+
+        def make_tables():
+            nc.vector.tensor_copy(
+                out=tables_bf16[:, 0, :, :, :], in_=cos_sb[:].unsqueeze(3).to_broadcast([P, SEQ_TILES, HALF, 2])
+            )
+            nc.vector.tensor_copy(out=tables_bf16[:, 1, :, :, 0], in_=sin_sb[:])
+            nc.vector.tensor_scalar_mul(out=tables_bf16[:, 1, :, :, 1], in0=sin_sb[:], scalar1=-1.0)
+
         tables = table_banks.tile([P, 2, SEQ_TILES, UNIT], F32)
 
         def tables_to_psum():
@@ -119,11 +136,12 @@ def tile_mla_pb_kernel(tc, x, wq_w_words, wq_w_scales, wq_b, cos, sin, out):
             )
 
         def spread_bias(nb):
+            row, first = nb * BLOCK // (N_OUT // 2), nb * BLOCK % (N_OUT // 2)
             bias_bank = banks.tile([P, BLOCK], F32, tag="bank")
             nc.tensor.matmul(
                 out=bias_bank[:],
-                lhsT=ident_bf16[:, nb : nb + 1].to_broadcast([P, P]),
-                rhs=bias_rows[:],
+                lhsT=ident_bf16[:, row : row + 1].to_broadcast([P, P]),
+                rhs=bias_rows[:, first : first + BLOCK],
                 start=True,
                 stop=True,
             )
@@ -150,16 +168,11 @@ def tile_mla_pb_kernel(tc, x, wq_w_words, wq_w_scales, wq_b, cos, sin, out):
             nc.vector.quantize_mx(out=x_codes[m][:].bitcast(FP8X4), scales=x_scales[m][:], in_=x_grouped[m][:])
 
         turn(0)
-        turn(1)
-        quantise(0)
-        tables_to_psum()
         for nb in block_order[:2]:
             spread_bias(nb)
-        turn(2)
+        quantise(0)
+        turn(1)
         quantise(1)
-        turn(3)
-        quantise(2)
-        quantise(3)
 
         q_tiles = {}
 
@@ -254,7 +267,8 @@ def tile_mla_pb_kernel(tc, x, wq_w_words, wq_w_scales, wq_b, cos, sin, out):
             else:
                 store_pieces(nc.sync, nb, m, pieces)
 
-        for job in jobs:
+        for i in range(len(jobs)):
+            job = jobs[i]
             nb, m, pieces = job
             ahead = block_order.index(nb) + 2
             if m == 1 and pieces is None and ahead < BLOCKS:
@@ -269,6 +283,16 @@ def tile_mla_pb_kernel(tc, x, wq_w_words, wq_w_scales, wq_b, cos, sin, out):
             if pieces == outer:
                 store_pieces(nc.scalar, nb, m, outer)
                 continue
-            if len(due) > 0:
-                rotate_next()
+            if i >= TOKEN_TILES:
+                for n in range(min(2, len(due))):
+                    rotate_next()
             due.extend([job])
+            if i == 1:
+                make_tables()
+            if i == TOKEN_TILES - 1:
+                tables_to_psum()
+            if i == 0:
+                turn(2)
+                turn(3)
+                quantise(2)
+                quantise(3)

@@ -65,7 +65,8 @@ def tile_mla_pb_kernel(tc, x, wq_w_words, wq_w_scales, wq_b, cos, sin, out):
             keep.tile([P, PASSES, BLOCK], U8, align_bytes=64, name="w_scales%d" % nb)
             for nb in range(BLOCKS)
         ]
-        bias_rows = keep.tile([P, N_OUT // 2], BF16)
+        late_blocks = BLOCKS - 2
+        bias_rows = [keep.tile([P, BLOCK], BF16, name="bias_rows%d" % i) for i in range(2)]
         bias_sb = [keep.tile([P, BLOCK], F32, name="bias_sb%d" % nb) for nb in range(BLOCKS)]
         ident_f32 = keep.tile([P, P], F32)
         ident_bf16 = keep.tile([P, P], BF16)
@@ -73,16 +74,13 @@ def tile_mla_pb_kernel(tc, x, wq_w_words, wq_w_scales, wq_b, cos, sin, out):
         sin_sb = keep.tile([P, SEQ_TILES, HALF], BF16)
         tables_bf16 = keep.tile([P, 2, SEQ_TILES, HALF, 2], BF16)
 
-        def zero_scales(engine, nb):
-            engine.memset(w_scales[nb][:].bitcast(F32), 0.0)
-
-        zero_scales(nc.vector, block_order[0])
-        nc.vector.memset(bias_rows[:].bitcast(I32), 0)
-        zero_scales(nc.vector, block_order[1])
+        nc.vector.memset(bias_rows[1][:].bitcast(I32), 0)
+        nc.vector.memset(w_scales[block_order[0]][:].bitcast(I32), 0)
+        nc.vector.memset(bias_rows[0][:].bitcast(I32), 0)
+        for nb in block_order[1:]:
+            nc.vector.memset(w_scales[nb][:].bitcast(I32), 0)
         make_identity(nc, ident_f32[:])
         make_identity(nc, ident_bf16[:])
-        for nb in block_order[2:]:
-            zero_scales(nc.gpsimd, nb)
 
         def load_x(m):
             width = DIM // x_pieces[m]
@@ -104,13 +102,15 @@ def tile_mla_pb_kernel(tc, x, wq_w_words, wq_w_scales, wq_b, cos, sin, out):
                 in_=wq_w_words[:, :, word_bytes].bitcast(I32).rearrange("g p b -> p g b"),
             )
 
+        bias_by_block = wq_b.rearrange("(r c) -> r c", c=BLOCK)
         load_x(0)
-        nc.sync.dma_start(out=bias_rows[0:2, :], in_=wq_b.rearrange("(r c) -> r c", r=2))
+        nc.scalar.dma_start(out=bias_rows[1][0 : BLOCKS - late_blocks, :], in_=bias_by_block[late_blocks:BLOCKS, :])
         load_scales(block_order[0])
         load_x(1)
         load_words(block_order[0])
         load_x(2)
         load_x(3)
+        nc.sync.dma_start(out=bias_rows[0][0:late_blocks, :], in_=bias_by_block[0:late_blocks, :])
         nc.sync.dma_start(out=cos_sb[:], in_=cos.rearrange("(t p) j -> p t j", p=P))
         nc.sync.dma_start(out=sin_sb[:], in_=sin.rearrange("(t p) j -> p t j", p=P))
         for nb in block_order[1:]:
@@ -136,12 +136,12 @@ def tile_mla_pb_kernel(tc, x, wq_w_words, wq_w_scales, wq_b, cos, sin, out):
             )
 
         def spread_bias(nb):
-            row, first = nb * BLOCK // (N_OUT // 2), nb * BLOCK % (N_OUT // 2)
+            early, row = divmod(nb, late_blocks)
             bias_bank = banks.tile([P, BLOCK], F32, tag="bank")
             nc.tensor.matmul(
                 out=bias_bank[:],
                 lhsT=ident_bf16[:, row : row + 1].to_broadcast([P, P]),
-                rhs=bias_rows[:, first : first + BLOCK],
+                rhs=bias_rows[early][:],
                 start=True,
                 stop=True,
             )

@@ -36,7 +36,7 @@ def tile_mla_pb_kernel(tc, x, wq_w_words, wq_w_scales, wq_b, cos, sin, out):
     nc = tc.nc
     x_rows = x.flatten_outer_dims()
     out_rows = out.rearrange("b s h d -> b s (h d)")
-    block_order = [5, 4, 2, 1, 3, 0]
+    block_order = [5, 4, 3, 2, 1, 0]
     last_block = block_order[-1]
     split_tiles = [2, 3]
 
@@ -65,18 +65,19 @@ def tile_mla_pb_kernel(tc, x, wq_w_words, wq_w_scales, wq_b, cos, sin, out):
             keep.tile([P, PASSES, BLOCK], U8, align_bytes=64, name="w_scales%d" % nb)
             for nb in range(BLOCKS)
         ]
-        late_blocks = BLOCKS - 2
-        bias_rows = [keep.tile([P, BLOCK], BF16, name="bias_rows%d" % i) for i in range(2)]
-        bias_sb = [keep.tile([P, BLOCK], F32, name="bias_sb%d" % nb) for nb in range(BLOCKS)]
+        late_blocks = BLOCKS - 3
+        first_row_block = BLOCKS - 4
+        bias_rows = keep.tile([P, BLOCK], BF16)
+        bias_late = keep.tile([P, late_blocks * BLOCK], BF16)
+        bias_early = [keep.tile([P, BLOCK], F32, name="bias_early%d" % i) for i in range(BLOCKS - late_blocks)]
         ident_f32 = keep.tile([P, P], F32)
         ident_bf16 = keep.tile([P, P], BF16)
         cos_sb = keep.tile([P, SEQ_TILES, HALF], BF16)
         sin_sb = keep.tile([P, SEQ_TILES, HALF], BF16)
         tables_bf16 = keep.tile([P, 2, SEQ_TILES, HALF, 2], BF16)
 
-        nc.vector.memset(bias_rows[1][:].bitcast(I32), 0)
+        nc.vector.memset(bias_rows[:].bitcast(I32), 0)
         nc.vector.memset(w_scales[block_order[0]][:].bitcast(I32), 0)
-        nc.vector.memset(bias_rows[0][:].bitcast(I32), 0)
         for nb in block_order[1:]:
             nc.vector.memset(w_scales[nb][:].bitcast(I32), 0)
         make_identity(nc, ident_f32[:])
@@ -104,13 +105,12 @@ def tile_mla_pb_kernel(tc, x, wq_w_words, wq_w_scales, wq_b, cos, sin, out):
 
         bias_by_block = wq_b.rearrange("(r c) -> r c", c=BLOCK)
         load_x(0)
-        nc.scalar.dma_start(out=bias_rows[1][0 : BLOCKS - late_blocks, :], in_=bias_by_block[late_blocks:BLOCKS, :])
+        nc.scalar.dma_start(out=bias_rows[0 : BLOCKS - first_row_block, :], in_=bias_by_block[first_row_block:BLOCKS, :])
         load_scales(block_order[0])
         load_x(1)
         load_words(block_order[0])
         load_x(2)
         load_x(3)
-        nc.sync.dma_start(out=bias_rows[0][0:late_blocks, :], in_=bias_by_block[0:late_blocks, :])
         nc.sync.dma_start(out=cos_sb[:], in_=cos.rearrange("(t p) j -> p t j", p=P))
         nc.sync.dma_start(out=sin_sb[:], in_=sin.rearrange("(t p) j -> p t j", p=P))
         for nb in block_order[1:]:
@@ -136,16 +136,21 @@ def tile_mla_pb_kernel(tc, x, wq_w_words, wq_w_scales, wq_b, cos, sin, out):
             )
 
         def spread_bias(nb):
-            early, row = divmod(nb, late_blocks)
+            row = nb - first_row_block
             bias_bank = banks.tile([P, BLOCK], F32, tag="bank")
             nc.tensor.matmul(
                 out=bias_bank[:],
                 lhsT=ident_bf16[:, row : row + 1].to_broadcast([P, P]),
-                rhs=bias_rows[early][:],
+                rhs=bias_rows[:],
                 start=True,
                 stop=True,
             )
-            nc.scalar.copy(out=bias_sb[nb][:], in_=bias_bank[:])
+            nc.scalar.copy(out=bias_early[nb - late_blocks][:], in_=bias_bank[:])
+
+        def bias_of(nb):
+            if nb < late_blocks:
+                return bias_late[:, nb * BLOCK : (nb + 1) * BLOCK]
+            return bias_early[nb - late_blocks][:]
 
         def turn(m):
             passes_in_piece = PASSES // x_pieces[m]
@@ -201,7 +206,7 @@ def tile_mla_pb_kernel(tc, x, wq_w_words, wq_w_scales, wq_b, cos, sin, out):
         def whole_block(nb, m):
             acc = banks.tile([P, BLOCK], F32, tag="bank")
             multiply(acc[:], nb, m, 0, BLOCK)
-            nc.vector.tensor_tensor(out=result_tile(nb, m, None), in0=acc[:], in1=bias_sb[nb][:], op=ADD)
+            nc.vector.tensor_tensor(out=result_tile(nb, m, None), in0=acc[:], in1=bias_of(nb), op=ADD)
 
         def both(pieces):
             return slice(pieces[0], pieces[1] + 1, pieces[1] - pieces[0])
@@ -213,7 +218,7 @@ def tile_mla_pb_kernel(tc, x, wq_w_words, wq_w_scales, wq_b, cos, sin, out):
             nc.vector.tensor_tensor(
                 out=result_tile(nb, m, pieces).rearrange("p (s c) -> p s c", c=PIECE),
                 in0=acc[:],
-                in1=bias_sb[nb][:].rearrange("p (s c) -> p s c", c=PIECE)[:, both(pieces), :],
+                in1=bias_of(nb).rearrange("p (s c) -> p s c", c=PIECE)[:, both(pieces), :],
                 op=ADD,
             )
 
@@ -270,9 +275,8 @@ def tile_mla_pb_kernel(tc, x, wq_w_words, wq_w_scales, wq_b, cos, sin, out):
         for i in range(len(jobs)):
             job = jobs[i]
             nb, m, pieces = job
-            ahead = block_order.index(nb) + 2
-            if m == 1 and pieces is None and ahead < BLOCKS:
-                spread_bias(block_order[ahead])
+            if i == 2:
+                spread_bias(block_order[2])
             if pieces == outer:
                 while len(due) > 0:
                     rotate_next()
@@ -296,3 +300,4 @@ def tile_mla_pb_kernel(tc, x, wq_w_words, wq_w_scales, wq_b, cos, sin, out):
                 turn(3)
                 quantise(2)
                 quantise(3)
+                nc.scalar.dma_start(out=bias_late[:], in_=wq_b[0 : late_blocks * BLOCK].partition_broadcast(P))

@@ -52,6 +52,8 @@ def tile_mla_pb_kernel(tc, x, wq_w_words, wq_w_scales, wq_b, cos, sin, out):
             [keep.tile([P, DIM // x_pieces[m]], BF16, name="x_sb%d_%d" % (m, i)) for i in range(x_pieces[m])]
             for m in range(TOKEN_TILES)
         ]
+        sorted_tiles = [2, 3]
+        x_sorted = [keep.tile([P, DIM // 2], F32, name="x_sorted%d" % m) for m in sorted_tiles]
         x_grouped = [
             keep.tile([P, PASSES * P * 4], BF16, align_bytes=64, name="x_grouped%d" % m) for m in range(TOKEN_TILES)
         ]
@@ -65,8 +67,7 @@ def tile_mla_pb_kernel(tc, x, wq_w_words, wq_w_scales, wq_b, cos, sin, out):
             keep.tile([P, PASSES, BLOCK], U8, align_bytes=64, name="w_scales%d" % nb)
             for nb in range(BLOCKS)
         ]
-        late_blocks = BLOCKS - 3
-        first_row_block = BLOCKS - 4
+        late_blocks = BLOCKS - 2
         bias_rows = keep.tile([P, BLOCK], BF16)
         bias_late = keep.tile([P, late_blocks * BLOCK], BF16)
         bias_early = [keep.tile([P, BLOCK], F32, name="bias_early%d" % i) for i in range(BLOCKS - late_blocks)]
@@ -105,7 +106,7 @@ def tile_mla_pb_kernel(tc, x, wq_w_words, wq_w_scales, wq_b, cos, sin, out):
 
         bias_by_block = wq_b.rearrange("(r c) -> r c", c=BLOCK)
         load_x(0)
-        nc.scalar.dma_start(out=bias_rows[0 : BLOCKS - first_row_block, :], in_=bias_by_block[first_row_block:BLOCKS, :])
+        nc.scalar.dma_start(out=bias_rows[0 : BLOCKS - late_blocks, :], in_=bias_by_block[late_blocks:BLOCKS, :])
         load_scales(block_order[0])
         load_x(1)
         load_words(block_order[0])
@@ -136,7 +137,7 @@ def tile_mla_pb_kernel(tc, x, wq_w_words, wq_w_scales, wq_b, cos, sin, out):
             )
 
         def spread_bias(nb):
-            row = nb - first_row_block
+            row = nb - late_blocks
             bias_bank = banks.tile([P, BLOCK], F32, tag="bank")
             nc.tensor.matmul(
                 out=bias_bank[:],
@@ -152,6 +153,16 @@ def tile_mla_pb_kernel(tc, x, wq_w_words, wq_w_scales, wq_b, cos, sin, out):
                 return bias_late[:, nb * BLOCK : (nb + 1) * BLOCK]
             return bias_early[nb - late_blocks][:]
 
+        def sort_words(m):
+            for half in range(PASSES // 2):
+                words = slice(512 * half, 512 * (half + 1))
+                src = x_sb[m][0][:].bitcast(F32)[:, words].rearrange("p (g q u) -> p g u q", g=2, u=2)
+                dst = x_sorted[sorted_tiles.index(m)][:, words].rearrange("p (g u q) -> p g u q", g=2, u=2)
+                if half == 0:
+                    nc.vector.tensor_copy(out=dst, in_=src)
+                else:
+                    nc.scalar.copy(out=dst, in_=src)
+
         def turn(m):
             passes_in_piece = PASSES // x_pieces[m]
             grouped_words = x_grouped[m][:].bitcast(F32)
@@ -159,9 +170,13 @@ def tile_mla_pb_kernel(tc, x, wq_w_words, wq_w_scales, wq_b, cos, sin, out):
                 turned = banks.tile([P, 4, P], F32, tag="bank")
                 for i in range(4):
                     g, u = 2 * half + i // 2, i % 2
-                    words = x_sb[m][g // passes_in_piece][:].bitcast(F32)
-                    first = 256 * (g % passes_in_piece)
-                    nc.tensor.transpose(turned[:, i, :], words[:, first + u : first + 256 : 2], ident_f32[:])
+                    if m in sorted_tiles:
+                        first = 256 * g + P * u
+                        words = x_sorted[sorted_tiles.index(m)][:, first : first + P]
+                    else:
+                        first = 256 * (g % passes_in_piece)
+                        words = x_sb[m][g // passes_in_piece][:].bitcast(F32)[:, first + u : first + 256 : 2]
+                    nc.tensor.transpose(turned[:, i, :], words, ident_f32[:])
                 dst = grouped_words[:, 512 * half : 512 * (half + 1)].rearrange("p (g r u) -> p g r u", g=2, u=2)
                 src = turned[:].rearrange("p (g u) r -> p g r u", u=2)
                 if half == 0:
@@ -178,6 +193,7 @@ def tile_mla_pb_kernel(tc, x, wq_w_words, wq_w_scales, wq_b, cos, sin, out):
         quantise(0)
         turn(1)
         quantise(1)
+        sort_words(2)
 
         q_tiles = {}
 
@@ -253,7 +269,11 @@ def tile_mla_pb_kernel(tc, x, wq_w_words, wq_w_scales, wq_b, cos, sin, out):
 
         middle = (1, 2)
         outer = (0, 3)
-        jobs = [(nb, m, None) for nb in block_order for m in range(TOKEN_TILES)]
+        first_nb, second_nb = block_order[0:2]
+        jobs = [(first_nb, 0, None), (first_nb, 1, None), (second_nb, 0, None)]
+        jobs.extend([(first_nb, 2, None), (first_nb, 3, None)])
+        jobs.extend([(second_nb, m, None) for m in range(1, TOKEN_TILES)])
+        jobs.extend([(nb, m, None) for nb in block_order[2:] for m in range(TOKEN_TILES)])
         jobs = jobs[: -len(split_tiles)]
         jobs.extend([(last_block, m, middle) for m in split_tiles])
         jobs.extend([(last_block, m, outer) for m in split_tiles])
@@ -275,8 +295,6 @@ def tile_mla_pb_kernel(tc, x, wq_w_words, wq_w_scales, wq_b, cos, sin, out):
         for i in range(len(jobs)):
             job = jobs[i]
             nb, m, pieces = job
-            if i == 2:
-                spread_bias(block_order[2])
             if pieces == outer:
                 while len(due) > 0:
                     rotate_next()
@@ -291,13 +309,14 @@ def tile_mla_pb_kernel(tc, x, wq_w_words, wq_w_scales, wq_b, cos, sin, out):
                 for n in range(min(2, len(due))):
                     rotate_next()
             due.extend([job])
-            if i == 1:
-                make_tables()
+            if i == 0:
+                sort_words(3)
+                nc.scalar.dma_start(out=bias_late[:], in_=wq_b[0 : late_blocks * BLOCK].partition_broadcast(P))
             if i == TOKEN_TILES - 1:
                 tables_to_psum()
-            if i == 0:
+            if i == 1:
                 turn(2)
                 turn(3)
                 quantise(2)
                 quantise(3)
-                nc.scalar.dma_start(out=bias_late[:], in_=wq_b[0 : late_blocks * BLOCK].partition_broadcast(P))
+                make_tables()

@@ -21,6 +21,7 @@ TOKEN_TILES = BATCH * SEQ // P
 SEQ_TILES = SEQ // P
 K_PASS = 4 * P
 PASSES = DIM // K_PASS
+HALVES = PASSES // 2
 BLOCK = 512
 BLOCKS = N_OUT // BLOCK
 UNIT = 64
@@ -55,10 +56,17 @@ def tile_mla_pb_kernel(tc, x, wq_w_words, wq_w_scales, wq_b, cos, sin, out):
         sorted_tiles = [2, 3]
         x_sorted = [keep.tile([P, DIM // 2], F32, name="x_sorted%d" % m) for m in sorted_tiles]
         x_grouped = [
-            keep.tile([P, PASSES * P * 4], BF16, align_bytes=64, name="x_grouped%d" % m) for m in range(TOKEN_TILES)
+            [keep.tile([P, 2 * P * 4], BF16, align_bytes=64, name="x_grouped%d_%d" % (m, h)) for h in range(HALVES)]
+            for m in range(TOKEN_TILES)
         ]
-        x_codes = [keep.tile([P, PASSES * P], U32, align_bytes=64, name="x_codes%d" % m) for m in range(TOKEN_TILES)]
-        x_scales = [keep.tile([P, PASSES * P], U8, align_bytes=64, name="x_scales%d" % m) for m in range(TOKEN_TILES)]
+        x_codes = [
+            [keep.tile([P, 2 * P], U32, align_bytes=64, name="x_codes%d_%d" % (m, h)) for h in range(HALVES)]
+            for m in range(TOKEN_TILES)
+        ]
+        x_scales = [
+            [keep.tile([P, 2 * P], U8, align_bytes=64, name="x_scales%d_%d" % (m, h)) for h in range(HALVES)]
+            for m in range(TOKEN_TILES)
+        ]
         w_words = [
             keep.tile([P, PASSES, 2 * BLOCK], U8, align_bytes=64, name="w_words%d" % nb)
             for nb in range(BLOCKS)
@@ -165,8 +173,7 @@ def tile_mla_pb_kernel(tc, x, wq_w_words, wq_w_scales, wq_b, cos, sin, out):
 
         def turn(m):
             passes_in_piece = PASSES // x_pieces[m]
-            grouped_words = x_grouped[m][:].bitcast(F32)
-            for half in range(PASSES // 2):
+            for half in range(HALVES):
                 turned = banks.tile([P, 4, P], F32, tag="bank")
                 for i in range(4):
                     g, u = 2 * half + i // 2, i % 2
@@ -177,7 +184,7 @@ def tile_mla_pb_kernel(tc, x, wq_w_words, wq_w_scales, wq_b, cos, sin, out):
                         first = 256 * (g % passes_in_piece)
                         words = x_sb[m][g // passes_in_piece][:].bitcast(F32)[:, first + u : first + 256 : 2]
                     nc.tensor.transpose(turned[:, i, :], words, ident_f32[:])
-                dst = grouped_words[:, 512 * half : 512 * (half + 1)].rearrange("p (g r u) -> p g r u", g=2, u=2)
+                dst = x_grouped[m][half][:].bitcast(F32).rearrange("p (g r u) -> p g r u", g=2, u=2)
                 src = turned[:].rearrange("p (g u) r -> p g r u", u=2)
                 if half == 0:
                     nc.vector.tensor_copy(out=dst, in_=src)
@@ -185,7 +192,10 @@ def tile_mla_pb_kernel(tc, x, wq_w_words, wq_w_scales, wq_b, cos, sin, out):
                     nc.scalar.copy(out=dst, in_=src)
 
         def quantise(m):
-            nc.vector.quantize_mx(out=x_codes[m][:].bitcast(FP8X4), scales=x_scales[m][:], in_=x_grouped[m][:])
+            for half in range(HALVES):
+                nc.vector.quantize_mx(
+                    out=x_codes[m][half][:].bitcast(FP8X4), scales=x_scales[m][half][:], in_=x_grouped[m][half][:]
+                )
 
         turn(0)
         for nb in block_order[:2]:
@@ -202,11 +212,11 @@ def tile_mla_pb_kernel(tc, x, wq_w_words, wq_w_scales, wq_b, cos, sin, out):
 
         def multiply(acc, nb, m, first, width):
             for g in range(PASSES):
-                toks = slice(g * P, (g + 1) * P)
+                half, toks = g // 2, slice(g % 2 * P, (g % 2 + 1) * P)
                 nc.tensor.matmul_mx(
                     out=acc,
-                    lhsT=x_codes[m][:, toks].bitcast(FP8X4),
-                    lhsT_scale=x_scales[m][:, toks],
+                    lhsT=x_codes[m][half][:, toks].bitcast(FP8X4),
+                    lhsT_scale=x_scales[m][half][:, toks],
                     rhs=w_words[nb][:, g, 2 * first : 2 * (first + width)].bitcast(FP4X4),
                     rhs_scale=w_scales[nb][:, g, first : first + width],
                     start=(g == 0),

@@ -120,11 +120,12 @@ def tile_mla_pb_kernel(tc, x, wq_w_words, wq_w_scales, wq_b, cos, sin, out):
         load_words(block_order[0])
         load_x(2)
         load_x(3)
-        nc.sync.dma_start(out=cos_sb[:], in_=cos.rearrange("(t p) j -> p t j", p=P))
-        nc.sync.dma_start(out=sin_sb[:], in_=sin.rearrange("(t p) j -> p t j", p=P))
         for nb in block_order[1:]:
             load_scales(nb)
             load_words(nb)
+            if nb == block_order[1]:
+                nc.sync.dma_start(out=cos_sb[:], in_=cos.rearrange("(t p) j -> p t j", p=P))
+                nc.sync.dma_start(out=sin_sb[:], in_=sin.rearrange("(t p) j -> p t j", p=P))
 
         def make_tables():
             nc.vector.tensor_copy(
@@ -321,7 +322,6 @@ def tile_mla_pb_kernel(tc, x, wq_w_words, wq_w_scales, wq_b, cos, sin, out):
             due.extend([job])
             if i == 0:
                 sort_words(3)
-                nc.scalar.dma_start(out=bias_late[:], in_=wq_b[0 : late_blocks * BLOCK].partition_broadcast(P))
             if i == TOKEN_TILES - 1:
                 tables_to_psum()
             if i == 1:
@@ -329,4 +329,5 @@ def tile_mla_pb_kernel(tc, x, wq_w_words, wq_w_scales, wq_b, cos, sin, out):
                 turn(3)
                 quantise(2)
                 quantise(3)
+                nc.scalar.dma_start(out=bias_late[:], in_=wq_b[0 : late_blocks * BLOCK].partition_broadcast(P))
                 make_tables()

from contextlib import ExitStack

import concourse.mybir as mybir
from concourse.masks import make_identity

F32 = mybir.dt.float32
BF16 = mybir.dt.bfloat16
I32 = mybir.dt.int32
U32 = mybir.dt.uint32
U8 = mybir.dt.uint8
FP8X4 = mybir.dt.float8_e4m3fn_x4
FP4X4 = mybir.dt.float4_e2m1fn_x4
ADD = mybir.AluOpType.add
MULT = mybir.AluOpType.mult

P = 128
BATCH, SEQ, DIM = 2, 256, 2048
HEADS, HEAD_DIM = 16, 192
N_OUT = HEADS * HEAD_DIM
TOKEN_TILES = BATCH * SEQ // P
SEQ_TILES = SEQ // P
K_PASS = 4 * P
PASSES = DIM // K_PASS
HALVES = PASSES // 2
BLOCK = 512
BLOCKS = N_OUT // BLOCK
UNIT = 64
UNITS = BLOCK // UNIT
MAX_ROT = 3
HALF = UNIT // 2
PIECE = 128

FLOPS = 2 * BATCH * SEQ * DIM * N_OUT


def tile_mla_pb_kernel(tc, x, wq_w_words, wq_w_scales, wq_b, cos, sin, out):
    nc = tc.nc
    x_rows = x.flatten_outer_dims()
    out_rows = out.rearrange("b s h d -> b s (h d)")
    block_order = [5, 4, 3, 2, 1, 0]
    last_block = block_order[-1]
    split_tiles = [2, 3]

    with ExitStack() as ctx:
        keep = ctx.enter_context(tc.tile_pool(name="keep", bufs=1))
        results = ctx.enter_context(tc.tile_pool(name="results", bufs=BLOCKS * TOKEN_TILES))
        banks = ctx.enter_context(tc.psum_pool(name="banks", bufs=7))
        table_banks = ctx.enter_context(tc.psum_pool(name="table_banks", bufs=1))
        ctx.enter_context(tc.manual_schedule())

        x_pieces = [2, 1, 1, 1]
        x_sb = [
            [keep.tile([P, DIM // x_pieces[m]], BF16, name="x_sb%d_%d" % (m, i)) for i in range(x_pieces[m])]
            for m in range(TOKEN_TILES)
        ]
        sorted_tiles = [2, 3]
        x_sorted = [keep.tile([P, DIM // 2], F32, name="x_sorted%d" % m) for m in sorted_tiles]
        x_grouped = [
            [keep.tile([P, 2 * P * 4], BF16, align_bytes=64, name="x_grouped%d_%d" % (m, h)) for h in range(HALVES)]
            for m in range(TOKEN_TILES)
        ]
        x_codes = [
            [keep.tile([P, 2 * P], U32, align_bytes=64, name="x_codes%d_%d" % (m, h)) for h in range(HALVES)]
            for m in range(TOKEN_TILES)
        ]
        x_scales = [
            [keep.tile([P, 2 * P], U8, align_bytes=64, name="x_scales%d_%d" % (m, h)) for h in range(HALVES)]
            for m in range(TOKEN_TILES)
        ]
        w_words = [
            keep.tile([P, PASSES, 2 * BLOCK], U8, align_bytes=64, name="w_words%d" % nb)
            for nb in range(BLOCKS)
        ]
        w_scales = [
            keep.tile([P, PASSES, BLOCK], U8, align_bytes=64, name="w_scales%d" % nb)
            for nb in range(BLOCKS)
        ]
        late_blocks = BLOCKS - 2
        bias_rows = keep.tile([P, BLOCK], BF16)
        bias_late = keep.tile([P, late_blocks * BLOCK], BF16)
        bias_early = [keep.tile([P, BLOCK], F32, name="bias_early%d" % i) for i in range(BLOCKS - late_blocks)]
        ident_f32 = keep.tile([P, P], F32)
        ident_bf16 = keep.tile([P, P], BF16)
        cos_sb = keep.tile([P, SEQ_TILES, HALF], BF16)
        sin_sb = keep.tile([P, SEQ_TILES, HALF], BF16)
        tables_bf16 = keep.tile([P, 2, SEQ_TILES, HALF, 2], BF16)

        nc.vector.memset(bias_rows[:].bitcast(I32), 0)
        nc.vector.memset(w_scales[block_order[0]][:].bitcast(I32), 0)
        for nb in block_order[1:]:
            nc.vector.memset(w_scales[nb][:].bitcast(I32), 0)
        make_identity(nc, ident_f32[:])
        make_identity(nc, ident_bf16[:])

        def load_x(m):
            width = DIM // x_pieces[m]
            for i in range(x_pieces[m]):
                nc.sync.dma_start(out=x_sb[m][i][:], in_=x_rows[m * P : (m + 1) * P, i * width : (i + 1) * width])

        def load_scales(nb):
            cols = slice(nb * BLOCK, (nb + 1) * BLOCK)
            for r in range(4):
                nc.sync.dma_start(
                    out=w_scales[nb][r:P:32, :, :].bitcast(I32),
                    in_=wq_w_scales[:, r:16:4, cols].bitcast(I32).rearrange("g q n -> q g n"),
                )

        def load_words(nb):
            word_bytes = slice(2 * nb * BLOCK, 2 * (nb + 1) * BLOCK)
            nc.sync.dma_start(
                out=w_words[nb][:].bitcast(I32),
                in_=wq_w_words[:, :, word_bytes].bitcast(I32).rearrange("g p b -> p g b"),
            )

        bias_by_block = wq_b.rearrange("(r c) -> r c", c=BLOCK)
        load_x(0)
        nc.scalar.dma_start(out=bias_rows[0 : BLOCKS - late_blocks, :], in_=bias_by_block[late_blocks:BLOCKS, :])
        load_scales(block_order[0])
        load_x(1)
        load_words(block_order[0])
        load_x(2)
        load_x(3)
        for nb in block_order[1:]:
            load_scales(nb)
            load_words(nb)
            if nb == block_order[1]:
                nc.sync.dma_start(out=cos_sb[:], in_=cos.rearrange("(t p) j -> p t j", p=P))
                nc.sync.dma_start(out=sin_sb[:], in_=sin.rearrange("(t p) j -> p t j", p=P))

        def make_tables():
            nc.vector.tensor_copy(
                out=tables_bf16[:, 0, :, :, :], in_=cos_sb[:].unsqueeze(3).to_broadcast([P, SEQ_TILES, HALF, 2])
            )
            nc.vector.tensor_copy(out=tables_bf16[:, 1, :, :, 0], in_=sin_sb[:])
            nc.vector.tensor_scalar_mul(out=tables_bf16[:, 1, :, :, 1], in0=sin_sb[:], scalar1=-1.0)

        tables = table_banks.tile([P, 2, SEQ_TILES, UNIT], F32)

        def tables_to_psum():
            nc.tensor.matmul(
                out=tables[:].rearrange("p w t c -> p (w t c)"),
                lhsT=ident_bf16[:],
                rhs=tables_bf16[:].rearrange("p w t j e -> p (w t j e)"),
                start=True,
                stop=True,
            )

        def spread_bias(nb):
            row = nb - late_blocks
            bias_bank = banks.tile([P, BLOCK], F32, tag="bank")
            nc.tensor.matmul(
                out=bias_bank[:],
                lhsT=ident_bf16[:, row : row + 1].to_broadcast([P, P]),
                rhs=bias_rows[:],
                start=True,
                stop=True,
            )
            nc.scalar.copy(out=bias_early[nb - late_blocks][:], in_=bias_bank[:])

        def bias_of(nb):
            if nb < late_blocks:
                return bias_late[:, nb * BLOCK : (nb + 1) * BLOCK]
            return bias_early[nb - late_blocks][:]

        def sort_words(m):
            for half in range(PASSES // 2):
                words = slice(512 * half, 512 * (half + 1))
                src = x_sb[m][0][:].bitcast(F32)[:, words].rearrange("p (g q u) -> p g u q", g=2, u=2)
                dst = x_sorted[sorted_tiles.index(m)][:, words].rearrange("p (g u q) -> p g u q", g=2, u=2)
                if half == 0:
                    nc.vector.tensor_copy(out=dst, in_=src)
                else:
                    nc.scalar.copy(out=dst, in_=src)

        def turn(m):
            passes_in_piece = PASSES // x_pieces[m]
            for half in range(HALVES):
                turned = banks.tile([P, 4, P], F32, tag="bank")
                for i in range(4):
                    g, u = 2 * half + i // 2, i % 2
                    if m in sorted_tiles:
                        first = 256 * g + P * u
                        words = x_sorted[sorted_tiles.index(m)][:, first : first + P]
                    else:
                        first = 256 * (g % passes_in_piece)
                        words = x_sb[m][g // passes_in_piece][:].bitcast(F32)[:, first + u : first + 256 : 2]
                    nc.tensor.transpose(turned[:, i, :], words, ident_f32[:])
                dst = x_grouped[m][half][:].bitcast(F32).rearrange("p (g r u) -> p g r u", g=2, u=2)
                src = turned[:].rearrange("p (g u) r -> p g r u", u=2)
                if half == 0:
                    nc.vector.tensor_copy(out=dst, in_=src)
                else:
                    nc.scalar.copy(out=dst, in_=src)

        def quantise(m):
            for half in range(HALVES):
                nc.vector.quantize_mx(
                    out=x_codes[m][half][:].bitcast(FP8X4), scales=x_scales[m][half][:], in_=x_grouped[m][half][:]
                )

        turn(0)
        for nb in block_order[:2]:
            spread_bias(nb)
        quantise(0)
        turn(1)
        quantise(1)
        sort_words(2)

        q_tiles = {}

        def rotated_units(nb):
            return slice((2 - UNITS * nb) % 3, UNITS, 3)

        def multiply(acc, nb, m, first, width):
            for g in range(PASSES):
                half, toks = g // 2, slice(g % 2 * P, (g % 2 + 1) * P)
                nc.tensor.matmul_mx(
                    out=acc,
                    lhsT=x_codes[m][half][:, toks].bitcast(FP8X4),
                    lhsT_scale=x_scales[m][half][:, toks],
                    rhs=w_words[nb][:, g, 2 * first : 2 * (first + width)].bitcast(FP4X4),
                    rhs_scale=w_scales[nb][:, g, first : first + width],
                    start=(g == 0),
                    stop=(g == PASSES - 1),
                )

        def result_tile(nb, m, pieces):
            if (nb, m, pieces) not in q_tiles:
                q_new = results.tile([P, BLOCK], F32, name="q")
                q_tiles[(nb, m, pieces)] = q_new
            return q_tiles[(nb, m, pieces)][:, 0 : BLOCK if pieces is None else 2 * PIECE]

        def whole_block(nb, m):
            acc = banks.tile([P, BLOCK], F32, tag="bank")
            multiply(acc[:], nb, m, 0, BLOCK)
            nc.vector.tensor_tensor(out=result_tile(nb, m, None), in0=acc[:], in1=bias_of(nb), op=ADD)

        def both(pieces):
            return slice(pieces[0], pieces[1] + 1, pieces[1] - pieces[0])

        def two_pieces(nb, m, pieces):
            acc = banks.tile([P, 2, PIECE], F32, tag="bank")
            for i in range(2):
                multiply(acc[:, i, :], nb, m, pieces[i] * PIECE, PIECE)
            nc.vector.tensor_tensor(
                out=result_tile(nb, m, pieces).rearrange("p (s c) -> p s c", c=PIECE),
                in0=acc[:],
                in1=bias_of(nb).rearrange("p (s c) -> p s c", c=PIECE)[:, both(pieces), :],
                op=ADD,
            )

        def store_pieces(queue, nb, m, pieces):
            b, t = m // SEQ_TILES, m % SEQ_TILES
            queue.dma_start(
                out=out_rows[b, t * P : (t + 1) * P, nb * BLOCK : (nb + 1) * BLOCK].rearrange(
                    "r (s c) -> r s c", c=PIECE
                )[:, both(pieces), :],
                in_=result_tile(nb, m, pieces).rearrange("p (s c) -> p s c", c=PIECE),
            )

        def rotate(nb, m, pieces):
            units = result_tile(nb, m, pieces).rearrange("p (u c) -> p u c", c=UNIT)
            rotated = units[:, rotated_units(nb) if pieces is None else slice(0, 4, 3), :]
            n_rot = rotated.shape[1]
            shape = [P, 2, n_rot, UNIT]
            products_tile = results.tile([P, 2, MAX_ROT, UNIT], F32, name="products")
            products = products_tile[:, :, 0:n_rot, :]
            nc.vector.tensor_tensor(
                out=products,
                in0=rotated.unsqueeze(1).to_broadcast(shape),
                in1=tables[:, :, m % SEQ_TILES, :].unsqueeze(2).to_broadcast(shape),
                op=MULT,
            )
            nc.gpsimd.tensor_tensor(
                out=rotated.rearrange("p u (j e) -> p u j e", e=2),
                in0=products[:, 0, :, :].rearrange("p u (j e) -> p u j e", e=2),
                in1=products[:, 1, :, :].rearrange("p u (j e) -> p u j e", e=2)[:, :, :, ::-1],
                op=ADD,
            )

        middle = (1, 2)
        outer = (0, 3)
        first_nb, second_nb = block_order[0:2]
        jobs = [(first_nb, 0, None), (first_nb, 1, None), (second_nb, 0, None)]
        jobs.extend([(first_nb, 2, None), (first_nb, 3, None)])
        jobs.extend([(second_nb, m, None) for m in range(1, TOKEN_TILES)])
        jobs.extend([(nb, m, None) for nb in block_order[2:] for m in range(TOKEN_TILES)])
        jobs = jobs[: -len(split_tiles)]
        jobs.extend([(last_block, m, middle) for m in split_tiles])
        jobs.extend([(last_block, m, outer) for m in split_tiles])
        due = []

        def rotate_next():
            nb, m, pieces = due[0]
            due.remove(due[0])
            rotate(nb, m, pieces)
            if pieces is None:
                b, t = m // SEQ_TILES, m % SEQ_TILES
                nc.sync.dma_start(
                    out=out_rows[b, t * P : (t + 1) * P, nb * BLOCK : (nb + 1) * BLOCK],
                    in_=result_tile(nb, m, None)
                )
            else:
                store_pieces(nc.sync, nb, m, pieces)

        for i in range(len(jobs)):
            job = jobs[i]
            nb, m, pieces = job
            if pieces == outer:
                while len(due) > 0:
                    rotate_next()
            if pieces is None:
                whole_block(nb, m)
            else:
                two_pieces(nb, m, pieces)
            if pieces == outer:
                store_pieces(nc.scalar, nb, m, outer)
                continue
            if i >= TOKEN_TILES:
                for n in range(min(2, len(due))):
                    rotate_next()
            due.extend([job])
            if i == 0:
                sort_words(3)
            if i == TOKEN_TILES - 1:
                tables_to_psum()
            if i == 1:
                turn(2)
                turn(3)
                quantise(2)
                quantise(3)
                nc.scalar.dma_start(out=bias_late[:], in_=wq_b[0 : late_blocks * BLOCK].partition_broadcast(P))
                make_tables()
